import numpy as np
import ml_dtypes


def mxq(x, axis, fmt="e4m3"):
    dtype, down = {"e4m3": (ml_dtypes.float8_e4m3fn, 7), "e5m2": (ml_dtypes.float8_e5m2, 14)}[fmt]
    v = np.moveaxis(np.asarray(x, np.float32).astype(ml_dtypes.bfloat16).astype(np.float64), axis, -1)
    blocks = v.reshape(v.shape[:-1] + (-1, 32))
    amax = np.abs(blocks).max(-1, keepdims=True)
    byte = np.maximum(np.where(amax > 0, np.frexp(amax)[1] - 1 + 127, 0) - down, 1)
    scale = np.exp2(byte - 127.0)
    codes = (blocks / scale).astype(np.float32).astype(dtype).astype(np.float64)
    return np.moveaxis((codes * scale).reshape(v.shape), -1, axis)


WIDE = False


def mx_kscale(k):
    if not WIDE:
        return np.ones(k)
    levels = np.array([30, -30])
    if k % 512:
        return np.exp2(np.random.permutation(np.resize(levels, k // 32))).repeat(32)
    a = np.empty((k // 512, 16))
    for p in range(k // 512):
        a[p, :8] = np.random.permutation(np.resize(levels, 8))
        for g in range(8):
            far = levels[np.abs(levels - a[p, g]) >= 10]
            a[p, g + 8] = far[np.random.randint(len(far))]
    return np.exp2(a.ravel()).repeat(32)


BF16 = ml_dtypes.bfloat16


def bf(x):
    return np.asarray(x, np.float32).astype(BF16)


def f64(x):
    return np.asarray(x).astype(np.float64)


B, D, H = 512, 1024, 1024
PASS = 512
MX_REC = H % PASS == 0


def sigmoid(v):
    return 1.0 / (1.0 + np.exp(-v))


def setup_inputs():
    s = mx_kscale(D)
    r = mx_kscale(H) if MX_REC else np.ones(H)
    gate_b = np.concatenate([np.zeros(H), np.zeros(H), np.ones(H), np.zeros(H)])
    return {"x_t": bf(np.random.standard_normal((B, D)) * s),
            "h_prev": bf(np.random.standard_normal((B, H)) * r),
            "c_prev": bf(np.random.standard_normal((B, H))),
            "n_prev": bf(0.5 + np.abs(np.random.standard_normal((B, H)))),
            "W": bf(np.random.standard_normal((D, 4 * H)) / np.sqrt(D) / s[:, None]),
            "R": bf(np.random.standard_normal((H, 4 * H)) / np.sqrt(H) / r[:, None]),
            "b": bf(gate_b + 0.2 * np.random.standard_normal(4 * H))}


def reference(x_t, h_prev, c_prev, n_prev, W, R, b):
    inp = mxq(f64(x_t), 1, "e5m2") @ mxq(f64(W), 0, "e5m2")
    if MX_REC:
        rec = mxq(f64(h_prev), 1, "e5m2") @ mxq(f64(R), 0, "e5m2")
    else:
        rec = f64(h_prev) @ f64(R)
    pre = inp + rec + f64(b)
    z_tilde, i_tilde, f_tilde, o_tilde = np.split(pre, 4, axis=-1)
    z_t = np.tanh(z_tilde)
    i_t = np.minimum(np.exp(i_tilde), 50.0)
    f_t = sigmoid(f_tilde)
    o_t = sigmoid(o_tilde)
    c_t = f_t * f64(c_prev) + i_t * z_t
    n_t = f_t * f64(n_prev) + i_t
    h_t = o_t * (c_t / (n_t + 1e-6))
    return h_t, c_t, n_t

@@ -1,0 +1,312 @@
+from contextlib import ExitStack
+
+import concourse.mybir as mybir
+from concourse.masks import make_identity
+
+F32 = mybir.dt.float32
+BF16 = mybir.dt.bfloat16
+U32 = mybir.dt.uint32
+U8 = mybir.dt.uint8
+E5M2X4 = mybir.dt.float8_e5m2_x4
+AF = mybir.ActivationFunctionType
+ALU = mybir.AluOpType
+
+B, D, H = 512, 1024, 1024
+FLOPS = 2 * B * (D + H) * 4 * H
+
+P = 128
+NBT = B // P
+HALF = 512
+GATE_ORDER = (2, 1, 0, 3)
+G_F, G_I, G_Z, G_O = 0, 1, 2, 3
+
+MANUAL = False
+RAW_BUFS = 8
+V_COLS = (512,512,512,512,176,176,176,176,176,176,176,176,176,176,176,176,256,256,256,256,256,256,256,256,512,512,512,512,512,176,176,176)
+EB = 19
+BL = 5
+R_LN = 24
+R_MX, R_ACT, R_MID, R_TR, R_FIN = 5, 6, 7, 7, 8
+
+
+def tile_slstmcell_kernel(tc, x_t, h_prev, c_prev, n_prev, W, R, b, out_0, out_1, out_2):
+    nc = tc.nc
+    with ExitStack() as ctx:
+        const = ctx.enter_context(tc.tile_pool(name="const", bufs=1))
+        keep = ctx.enter_context(tc.tile_pool(name="keep", bufs=1))
+        rawp = ctx.enter_context(tc.tile_pool(name="rawp", bufs=RAW_BUFS))
+        xinp = ctx.enter_context(tc.tile_pool(name="xinp", bufs=2))
+        grpp = ctx.enter_context(tc.tile_pool(name="grpp", bufs=4))
+        codp = ctx.enter_context(tc.tile_pool(name="codp", bufs=4))
+        gp = ctx.enter_context(tc.tile_pool(name="gp", bufs=3))
+        izp = ctx.enter_context(tc.tile_pool(name="izp", bufs=3))
+        hsp = ctx.enter_context(tc.tile_pool(name="hsp", bufs=2))
+        mxp = ctx.enter_context(tc.psum_pool(name="mxp", bufs=4))
+        tpp = ctx.enter_context(tc.psum_pool(name="tpp", bufs=4))
+        if MANUAL:
+            ctx.enter_context(tc.manual_schedule())
+
+        warm = const.tile([P, 1], F32, name="warm")
+        nc.vector.memset(warm[:], 0.0)
+        nc.scalar.activation(out=warm[:], in_=warm[:], func=AF.Exp)
+        ident = const.tile([P, P], F32, name="ident")
+        make_identity(nc, ident[:])
+        identb = const.tile([P, P], BF16, name="identb")
+        make_identity(nc, identb[:])
+        brow = const.tile([P, P], BF16, name="brow")
+        nc.gpsimd.memset(brow[:], 0.0)
+        nc.scalar.dma_start(out=brow[0:32, :], in_=b.rearrange("(t c) -> t c", c=P))
+
+        c_sb = keep.tile([P, NBT, H], BF16, name="c_sb")
+        n_sb = keep.tile([P, NBT, H], BF16, name="n_sb")
+        fc = keep.tile([P, NBT, H], F32, name="fc")
+        fn = keep.tile([P, NBT, H], F32, name="fn")
+        rr = keep.tile([P, NBT, H], F32, name="rr")
+        e_all = keep.tile([P, 8, B], F32, name="e_all")
+        xc = keep.tile([P, 4, B], U32, name="xc", align_bytes=64)
+        xs = keep.tile([P, 4, B], U8, name="xs", align_bytes=64)
+        bias = const.tile([P, 32], F32, name="bias")
+        bhalf = const.tile([P, 16], F32, name="bhalf")
+
+        c_view = c_prev.rearrange("(t p) c -> p t c", p=P)
+        n_view = n_prev.rearrange("(t p) c -> p t c", p=P)
+        out_views = [o.rearrange("(t p) c -> p t c", p=P) for o in (out_0, out_1, out_2)]
+
+        raw_of = {}
+        grp_of = {}
+        cod_of = {}
+        acc_of = {}
+        g_of = {}
+        tp_of = {}
+        hs_of = {}
+        xin_of = {}
+        xt_of = {}
+        gx_of = {}
+
+        def load_unit(u):
+            s, a = divmod(u, 4)
+            col0 = GATE_ORDER[s // 2] * H + (s % 2) * HALF
+            src = W if a < 2 else R
+            rows = src[(a % 2) * 512:(a % 2) * 512 + 512, col0:col0 + HALF]
+            raw = rawp.tile([P, 4, HALF], BF16, name="raw")
+            nc.sync.dma_start(out=raw[:], in_=rows.rearrange("(p j) w -> p j w", j=4))
+            raw_of[u] = raw
+
+        def interleave(u):
+            grp = grpp.tile([P, HALF, 4], BF16, name="grp", align_bytes=64)
+            src = raw_of.pop(u)[:].rearrange("p j w -> p w j")
+            vc = V_COLS[u]
+            if vc > 0:
+                nc.vector.tensor_copy(out=grp[:, 0:vc, :], in_=src[:, 0:vc, :])
+            if vc < HALF:
+                nc.scalar.copy(out=grp[:, vc:HALF, :], in_=src[:, vc:HALF, :])
+            grp_of[u] = grp
+
+        def quantise(u):
+            s, a = divmod(u, 4)
+            if a == 0:
+                cod = codp.tile([P, 4, HALF], U32, name="cod", align_bytes=64)
+                scl = codp.tile([P, 4, HALF], U8, name="scl", align_bytes=64)
+                cod_of[s] = (cod, scl)
+            cod, scl = cod_of[s]
+            nc.vector.quantize_mx(
+                out=cod[:, a, :].bitcast(E5M2X4),
+                scales=scl[:, a, :],
+                in_=grp_of.pop(u)[:].rearrange("p w j -> p (w j)"),
+            )
+
+        def load_x(i, bp):
+            if bp == 0:
+                xin = xinp.tile([P, NBT, D], BF16, name="xin")
+                xin_of[i] = xin
+            view = (x_t, h_prev)[i].rearrange("(t p) k -> p t k", p=P)
+            nc.sync.dma_start(out=xin_of[i][:, 2 * bp:2 * bp + 2, :], in_=view[:, 2 * bp:2 * bp + 2, :])
+
+        def x_transpose(i, bp):
+            words = xin_of[i][:].bitcast(F32)
+            for g in range(2):
+                xt = tpp.tile([P, 2, 256], F32, name="xt", tag="tp")
+                for u in range(2):
+                    for bl in range(2):
+                        nc.tensor.transpose(
+                            xt[:, u, bl * P:(bl + 1) * P],
+                            words[:, 2 * bp + bl, 256 * g + u:256 * (g + 1):2],
+                            ident[:],
+                        )
+                a = 2 * i + g
+                if bp == 0:
+                    gx = grpp.tile([P, B, 4], BF16, name="gx", tag="grp", align_bytes=64)
+                    gx_of[a] = gx
+                gw = gx_of[a][:].rearrange("p r t -> p (r t)").bitcast(F32).rearrange("p (r u) -> p r u", u=2)
+                nc.scalar.copy(out=gw[:, bp * 256:(bp + 1) * 256, :], in_=xt[:].rearrange("p u r -> p r u"))
+
+        def x_quantise(a):
+            nc.vector.quantize_mx(
+                out=xc[:, a, :].bitcast(E5M2X4),
+                scales=xs[:, a, :],
+                in_=gx_of.pop(a)[:].rearrange("p r t -> p (r t)"),
+            )
+
+        def load_cn(half):
+            cols = slice(half * HALF, (half + 1) * HALF)
+            nc.sync.dma_start(out=c_sb[:, :, cols], in_=c_view[:, :, cols])
+            nc.sync.dma_start(out=n_sb[:, :, cols], in_=n_view[:, :, cols])
+
+        def halve_n(half):
+            cols = slice(half * HALF, (half + 1) * HALF)
+            nc.vector.tensor_scalar_mul(out=n_sb[:, :, cols], in0=n_sb[:, :, cols], scalar1=0.5)
+
+        def where(e):
+            s = e // 4
+            return s // 2, (s % 2) * 4 + e % 4
+
+        def mx(e):
+            cod, scl = cod_of[e // 4]
+            cl = slice((e % 4) * P, (e % 4 + 1) * P)
+            acc = mxp.tile([P, B], F32, name="acc")
+            for a in range(4):
+                nc.tensor.matmul_mx(
+                    out=acc[:],
+                    lhsT=cod[:, a, cl].bitcast(E5M2X4),
+                    lhsT_scale=scl[:, a, cl],
+                    rhs=xc[:, a, :].bitcast(E5M2X4),
+                    rhs_scale=xs[:, a, :],
+                    start=(a == 0),
+                    stop=(a == 3),
+                )
+            acc_of[e] = acc
+
+        def act(e):
+            q, ct = where(e)
+            acc = acc_of.pop(e)
+            if q == G_I:
+                nc.scalar.activation(out=e_all[:, ct, :], in_=acc[:], func=AF.Exp,
+                                     bias=bias[:, 8 + ct:9 + ct], scale=1.0)
+                return
+            g = gp.tile([P, B], F32, name="g")
+            if q == G_Z:
+                nc.scalar.activation(out=g[:], in_=acc[:], func=AF.Tanh, bias=bias[:, ct:ct + 1], scale=1.0)
+            else:
+                col = ct if q == G_F else 8 + ct
+                nc.scalar.activation(out=g[:], in_=acc[:], func=AF.Tanh, bias=bhalf[:, col:col + 1], scale=0.5)
+            g_of[e] = g
+
+        def mid(e):
+            q, ct = where(e)
+            iz = izp.tile([P, B], F32, name="iz")
+            nc.vector.scalar_tensor_tensor(out=iz[:], in0=e_all[:, ct, :], scalar=50.0, in1=g_of.pop(e)[:],
+                                           op0=ALU.min, op1=ALU.mult)
+            g_of[e] = iz
+
+        def tr(e):
+            q, ct = where(e)
+            src = e_all[:, ct, :] if q == G_I else g_of.pop(e)[:]
+            tp = tpp.tile([P, NBT, P], F32, name="tp")
+            for bt in range(NBT):
+                nc.tensor.transpose(tp[:, bt, :], src[:, bt * P:(bt + 1) * P], ident[:])
+            tp_of[e] = tp
+
+        def fin(e):
+            q, ct = where(e)
+            cs = slice(ct * P, (ct + 1) * P)
+            tp = tp_of.pop(e)
+            if q == G_F:
+                nc.vector.scalar_tensor_tensor(out=fc[:, :, cs], in0=tp[:], scalar=1.0, in1=c_sb[:, :, cs],
+                                               op0=ALU.add, op1=ALU.mult)
+                nc.vector.scalar_tensor_tensor(out=fn[:, :, cs], in0=tp[:], scalar=1.0, in1=n_sb[:, :, cs],
+                                               op0=ALU.add, op1=ALU.mult)
+            elif q == G_I:
+                nc.vector.scalar_tensor_tensor(out=fn[:, :, cs], in0=tp[:], scalar=50.0, in1=fn[:, :, cs],
+                                               op0=ALU.min, op1=ALU.add)
+            elif q == G_Z:
+                nc.vector.scalar_tensor_tensor(out=fc[:, :, cs], in0=fc[:, :, cs], scalar=0.5, in1=tp[:],
+                                               op0=ALU.mult, op1=ALU.add)
+            else:
+                pair, lo = divmod(ct, 2)
+                if lo == 0:
+                    hs = hsp.tile([P, NBT, 2 * P], F32, name="hs")
+                    hs_of[pair] = hs
+                hs = hs_of[pair]
+                nc.vector.scalar_tensor_tensor(out=hs[:, :, lo * P:(lo + 1) * P], in0=tp[:], scalar=1.0,
+                                               in1=fc[:, :, cs], op0=ALU.add, op1=ALU.mult)
+                if lo == 1:
+                    pc = slice(pair * 2 * P, (pair + 1) * 2 * P)
+                    nc.vector.scalar_tensor_tensor(out=hs[:], in0=hs[:], scalar=0.5, in1=rr[:, :, pc],
+                                                   op0=ALU.mult, op1=ALU.mult)
+                    nc.sync.dma_start(out=out_views[0][:, :, pc], in_=hs[:])
+            if q in (G_I, G_Z) and ct % 4 == 3:
+                hc = slice((ct // 4) * HALF, (ct // 4 + 1) * HALF)
+                if q == G_I:
+                    nc.sync.dma_start(out=out_views[2][:, :, hc], in_=fn[:, :, hc])
+                else:
+                    nc.sync.dma_start(out=out_views[1][:, :, hc], in_=fc[:, :, hc])
+
+        def reciprocal_of_n():
+            for k in range(2):
+                nc.scalar.activation(out=rr[:, 2 * k:2 * k + 2, :], in_=fn[:, 2 * k:2 * k + 2, :], func=AF.Ln,
+                                     bias=1e-6, scale=1.0)
+            for k in range(2):
+                nc.scalar.activation(out=rr[:, 2 * k:2 * k + 2, :], in_=rr[:, 2 * k:2 * k + 2, :], func=AF.Exp,
+                                     scale=-1.0)
+
+        load_unit(0)
+        load_x(0, 0)
+        load_x(0, 1)
+        load_unit(1)
+        load_x(1, 0)
+        load_x(1, 1)
+        load_unit(2)
+        load_unit(3)
+        load_cn(0)
+        for u in range(4, RAW_BUFS):
+            load_unit(u)
+        load_cn(1)
+
+        bps = tpp.tile([P, P], BF16, name="bps", tag="tp")
+        nc.tensor.transpose(bps[:], brow[:], identb[:])
+        nc.vector.tensor_copy(out=bias[:], in_=bps[:, 0:32])
+        nc.vector.tensor_scalar_mul(out=bhalf[:], in0=bps[:, 16:32], scalar1=0.5)
+
+        def shifted(e):
+            return BL if e >= EB else 0
+
+        def items(r, base, only_z=None):
+            found = []
+            for e in range(32):
+                z = where(e)[0] == G_Z
+                extra = 1 if (z and only_z is False) else 0
+                if only_z is True and not z:
+                    continue
+                if e + base + extra + shifted(e) == r:
+                    found.append(e)
+            return found
+
+        last_round = 31 + R_FIN + 1 + BL
+        for r in range(last_round + 1):
+            for e in items(r, R_ACT):
+                act(e)
+            if r == R_LN:
+                reciprocal_of_n()
+            if r < 4:
+                x_transpose(r // 2, r % 2)
+            for e in items(r, R_TR, False):
+                tr(e)
+            for e in items(r, R_MX):
+                mx(e)
+            if r in (1, 3):
+                x_quantise(r - 1)
+                x_quantise(r)
+            if r < 32:
+                interleave(r)
+                if r + RAW_BUFS < 32:
+                    load_unit(r + RAW_BUFS)
+            if r == 5:
+                halve_n(0)
+            if r == 9:
+                halve_n(1)
+            for e in items(r, R_MID, True):
+                mid(e)
+            for e in items(r, R_FIN, False):
+                fin(e)
+            if 1 <= r <= 32:
+                quantise(r - 1)

@@ -94,12 +94,14 @@ def tile_slstmcell_kernel(tc, x_t, h_prev, c_prev, n_prev, W, R, b, out_0, out_1
 
         def interleave(u):
             grp = grpp.tile([P, HALF, 4], BF16, name="grp", align_bytes=64)
-            src = raw_of.pop(u)[:].rearrange("p j w -> p w j")
+            raw = raw_of.pop(u)
             vc = V_COLS[u]
             if vc > 0:
-                nc.vector.tensor_copy(out=grp[:, 0:vc, :], in_=src[:, 0:vc, :])
+                nc.vector.tensor_copy(out=grp[:, 0:vc, :].rearrange("p (c i) t -> p c t i", i=4),
+                                      in_=raw[:, :, 0:vc].rearrange("p t (c i) -> p c t i", i=4))
             if vc < HALF:
-                nc.scalar.copy(out=grp[:, vc:HALF, :], in_=src[:, vc:HALF, :])
+                nc.scalar.copy(out=grp[:, vc:HALF, :].rearrange("p (c i) t -> p c t i", i=4),
+                               in_=raw[:, :, vc:HALF].rearrange("p t (c i) -> p c t i", i=4))
             grp_of[u] = grp
 
         def quantise(u):

@@ -22,11 +22,18 @@ G_F, G_I, G_Z, G_O = 0, 1, 2, 3
 
 MANUAL = False
 RAW_BUFS = 8
-V_COLS = (512,512,512,512,176,176,176,176,176,176,176,176,176,176,176,176,256,256,256,256,256,256,256,256,512,512,512,512,512,176,176,176)
-EB = 19
-BL = 5
-R_LN = 24
-R_MX, R_ACT, R_MID, R_TR, R_FIN = 5, 6, 7, 7, 8
+GRP_BUFS = 5
+COD_BUFS = 3
+G_BUFS = 6
+IZ_BUFS = 3
+V_COLS = (512,512,512,512,128,128,96,96,96,96,96,96,96,96,160,160,160,160,160,160,160,160,96,512,512,512,512,96,96,96,96,96)
+PE_UNITS = (4, 6, 8, 10, 12, 14, 16, 18, 20, 22, 27, 29)
+LEAD = 6
+SLEAD = 1
+ML = 1
+CN1_AT = 10
+CR_SLOTS = (22, 26)
+LN_SLOT = 15
 
 
 def tile_slstmcell_kernel(tc, x_t, h_prev, c_prev, n_prev, W, R, b, out_0, out_1, out_2):
@@ -36,10 +43,11 @@ def tile_slstmcell_kernel(tc, x_t, h_prev, c_prev, n_prev, W, R, b, out_0, out_1
         keep = ctx.enter_context(tc.tile_pool(name="keep", bufs=1))
         rawp = ctx.enter_context(tc.tile_pool(name="rawp", bufs=RAW_BUFS))
         xinp = ctx.enter_context(tc.tile_pool(name="xinp", bufs=2))
-        grpp = ctx.enter_context(tc.tile_pool(name="grpp", bufs=4))
-        codp = ctx.enter_context(tc.tile_pool(name="codp", bufs=4))
-        gp = ctx.enter_context(tc.tile_pool(name="gp", bufs=3))
-        izp = ctx.enter_context(tc.tile_pool(name="izp", bufs=3))
+        gxp = ctx.enter_context(tc.tile_pool(name="gxp", bufs=2))
+        grpp = ctx.enter_context(tc.tile_pool(name="grpp", bufs=GRP_BUFS))
+        codp = ctx.enter_context(tc.tile_pool(name="codp", bufs=COD_BUFS))
+        gp = ctx.enter_context(tc.tile_pool(name="gp", bufs=G_BUFS))
+        izp = ctx.enter_context(tc.tile_pool(name="izp", bufs=IZ_BUFS))
         hsp = ctx.enter_context(tc.tile_pool(name="hsp", bufs=2))
         mxp = ctx.enter_context(tc.psum_pool(name="mxp", bufs=4))
         tpp = ctx.enter_context(tc.psum_pool(name="tpp", bufs=4))
@@ -47,16 +55,11 @@ def tile_slstmcell_kernel(tc, x_t, h_prev, c_prev, n_prev, W, R, b, out_0, out_1
             ctx.enter_context(tc.manual_schedule())
 
         warm = const.tile([P, 1], F32, name="warm")
-        nc.vector.memset(warm[:], 0.0)
-        nc.scalar.activation(out=warm[:], in_=warm[:], func=AF.Exp)
         ident = const.tile([P, P], F32, name="ident")
-        make_identity(nc, ident[:])
         identb = const.tile([P, P], BF16, name="identb")
-        make_identity(nc, identb[:])
         brow = const.tile([P, P], BF16, name="brow")
-        nc.gpsimd.memset(brow[:], 0.0)
-        nc.scalar.dma_start(out=brow[0:32, :], in_=b.rearrange("(t c) -> t c", c=P))
-
+        bias = const.tile([P, 32], F32, name="bias")
+        bhalf = const.tile([P, 16], F32, name="bhalf")
         c_sb = keep.tile([P, NBT, H], BF16, name="c_sb")
         n_sb = keep.tile([P, NBT, H], BF16, name="n_sb")
         fc = keep.tile([P, NBT, H], F32, name="fc")
@@ -65,67 +68,113 @@ def tile_slstmcell_kernel(tc, x_t, h_prev, c_prev, n_prev, W, R, b, out_0, out_1
         e_all = keep.tile([P, 8, B], F32, name="e_all")
         xc = keep.tile([P, 4, B], U32, name="xc", align_bytes=64)
         xs = keep.tile([P, 4, B], U8, name="xs", align_bytes=64)
-        bias = const.tile([P, 32], F32, name="bias")
-        bhalf = const.tile([P, 16], F32, name="bhalf")
 
-        c_view = c_prev.rearrange("(t p) c -> p t c", p=P)
-        n_view = n_prev.rearrange("(t p) c -> p t c", p=P)
-        out_views = [o.rearrange("(t p) c -> p t c", p=P) for o in (out_0, out_1, out_2)]
+        c_view = c_prev.rearrange("(p t) c -> p t c", t=NBT)
+        n_view = n_prev.rearrange("(p t) c -> p t c", t=NBT)
+        out_views = [o.rearrange("(p t) c -> p t c", t=NBT) for o in (out_0, out_1, out_2)]
 
-        raw_of = {}
-        grp_of = {}
-        cod_of = {}
-        acc_of = {}
-        g_of = {}
-        tp_of = {}
-        hs_of = {}
-        xin_of = {}
-        xt_of = {}
-        gx_of = {}
+        live = {}
 
-        def load_unit(u):
+        def where(e):
+            s = e // 4
+            return s // 2, (s % 2) * 4 + e % 4
+
+        def ld(u):
             s, a = divmod(u, 4)
             col0 = GATE_ORDER[s // 2] * H + (s % 2) * HALF
-            src = W if a < 2 else R
-            rows = src[(a % 2) * 512:(a % 2) * 512 + 512, col0:col0 + HALF]
+            rows = (W if a < 2 else R)[(a % 2) * 512:(a % 2) * 512 + 512, col0:col0 + HALF]
             raw = rawp.tile([P, 4, HALF], BF16, name="raw")
             nc.sync.dma_start(out=raw[:], in_=rows.rearrange("(p j) w -> p j w", j=4))
-            raw_of[u] = raw
+            live["raw", u] = raw
 
-        def interleave(u):
-            grp = grpp.tile([P, HALF, 4], BF16, name="grp", align_bytes=64)
-            raw = raw_of.pop(u)
+        def ldx(i, bp):
+            if bp == 0:
+                xin = xinp.tile([P, NBT, D], BF16, name="xin")
+                live["xin", i] = xin
+            view = (x_t, h_prev)[i].rearrange("(p t) k -> p t k", t=NBT)
+            nc.sync.dma_start(out=live["xin", i][:, 2 * bp:2 * bp + 2, :], in_=view[:, 2 * bp:2 * bp + 2, :])
+
+        def ldcn(half):
+            cols = slice(half * HALF, (half + 1) * HALF)
+            nc.sync.dma_start(out=c_sb[:, :, cols], in_=c_view[:, :, cols])
+            nc.sync.dma_start(out=n_sb[:, :, cols], in_=n_view[:, :, cols])
+
+        def stn(half):
+            hc = slice(half * HALF, (half + 1) * HALF)
+            nc.sync.dma_start(out=out_views[2][:, :, hc], in_=fn[:, :, hc])
+
+        def stc(half):
+            hc = slice(half * HALF, (half + 1) * HALF)
+            nc.sync.dma_start(out=out_views[1][:, :, hc], in_=fc[:, :, hc])
+
+        def sth(pair):
+            pc = slice(pair * 2 * P, (pair + 1) * 2 * P)
+            nc.sync.dma_start(out=out_views[0][:, :, pc], in_=live.pop(("hs", pair))[:])
+
+        def grp_tile(u):
+            if ("grp", u) not in live:
+                grp = grpp.tile([P, HALF, 4], BF16, name="grp", align_bytes=64)
+                live["grp", u] = grp
+            return live["grp", u]
+
+        def ilv(u):
             vc = V_COLS[u]
-            if vc > 0:
-                nc.vector.tensor_copy(out=grp[:, 0:vc, :].rearrange("p (c i) t -> p c t i", i=4),
-                                      in_=raw[:, :, 0:vc].rearrange("p t (c i) -> p c t i", i=4))
-            if vc < HALF:
-                nc.scalar.copy(out=grp[:, vc:HALF, :].rearrange("p (c i) t -> p c t i", i=4),
-                               in_=raw[:, :, vc:HALF].rearrange("p t (c i) -> p c t i", i=4))
-            grp_of[u] = grp
+            nc.vector.tensor_copy(out=grp_tile(u)[:, 0:vc, :].rearrange("p (c i) t -> p c t i", i=4),
+                                  in_=live["raw", u][:, :, 0:vc].rearrange("p t (c i) -> p c t i", i=4))
 
-        def quantise(u):
+        def ils(u):
+            vc = V_COLS[u]
+            nc.scalar.copy(out=grp_tile(u)[:, vc:HALF, :].rearrange("p (c i) t -> p c t i", i=4),
+                           in_=live["raw", u][:, :, vc:HALF].rearrange("p t (c i) -> p c t i", i=4))
+
+        def pil(u):
+            src = live["raw", u][:].rearrange("p j w -> p w j")
+            for k in range(2):
+                il = tpp.tile([P, 256, 4], BF16, name="il", tag="tp")
+                for m in range(2):
+                    w0 = 256 * k + 128 * m
+                    nc.tensor.matmul(out=il[:, 128 * m:128 * (m + 1), :], lhsT=identb[:], rhs=src[:, w0:w0 + 128, :],
+                                     start=True, stop=True)
+                live["il", u, k] = il
+
+        def pev(u):
+            for k in range(2):
+                nc.scalar.copy(out=grp_tile(u)[:, 256 * k:256 * (k + 1), :], in_=live.pop(("il", u, k))[:])
+
+        def q(u):
             s, a = divmod(u, 4)
             if a == 0:
                 cod = codp.tile([P, 4, HALF], U32, name="cod", align_bytes=64)
                 scl = codp.tile([P, 4, HALF], U8, name="scl", align_bytes=64)
-                cod_of[s] = (cod, scl)
-            cod, scl = cod_of[s]
+                live["cod", s] = (cod, scl)
+            cod, scl = live["cod", s]
             nc.vector.quantize_mx(
                 out=cod[:, a, :].bitcast(E5M2X4),
                 scales=scl[:, a, :],
-                in_=grp_of.pop(u)[:].rearrange("p w j -> p (w j)"),
+                in_=live.pop(("grp", u))[:].rearrange("p w j -> p (w j)"),
             )
+            live.pop(("raw", u))
 
-        def load_x(i, bp):
-            if bp == 0:
-                xin = xinp.tile([P, NBT, D], BF16, name="xin")
-                xin_of[i] = xin
-            view = (x_t, h_prev)[i].rearrange("(t p) k -> p t k", p=P)
-            nc.sync.dma_start(out=xin_of[i][:, 2 * bp:2 * bp + 2, :], in_=view[:, 2 * bp:2 * bp + 2, :])
+        def setup():
+            nc.vector.memset(warm[:], 0.0)
+            nc.scalar.activation(out=warm[:], in_=warm[:], func=AF.Exp)
+            make_identity(nc, ident[:])
+            make_identity(nc, identb[:])
+            nc.gpsimd.memset(brow[:], 0.0)
+            nc.sync.dma_start(out=brow[0:32, :], in_=b.rearrange("(t c) -> t c", c=P))
 
-        def x_transpose(i, bp):
-            words = xin_of[i][:].bitcast(F32)
+        def bT():
+            bps = tpp.tile([P, P], BF16, name="bps", tag="tp")
+            nc.tensor.transpose(bps[:], brow[:], identb[:])
+            live["bps"] = bps
+
+        def bcol():
+            bps = live.pop("bps")
+            nc.vector.tensor_copy(out=bias[:], in_=bps[:, 0:32])
+            nc.vector.tensor_scalar_mul(out=bhalf[:], in0=bps[:, 16:32], scalar1=0.5)
+
+        def xT(i, bp):
+            words = live["xin", i][:].bitcast(F32)
             for g in range(2):
                 xt = tpp.tile([P, 2, 256], F32, name="xt", tag="tp")
                 for u in range(2):
@@ -135,40 +184,40 @@ def tile_slstmcell_kernel(tc, x_t, h_prev, c_prev, n_prev, W, R, b, out_0, out_1
                             words[:, 2 * bp + bl, 256 * g + u:256 * (g + 1):2],
                             ident[:],
                         )
+                live["xt", i, bp, g] = xt
+
+        def xev(i, bp):
+            for g in range(2):
                 a = 2 * i + g
                 if bp == 0:
-                    gx = grpp.tile([P, B, 4], BF16, name="gx", tag="grp", align_bytes=64)
-                    gx_of[a] = gx
-                gw = gx_of[a][:].rearrange("p r t -> p (r t)").bitcast(F32).rearrange("p (r u) -> p r u", u=2)
-                nc.scalar.copy(out=gw[:, bp * 256:(bp + 1) * 256, :], in_=xt[:].rearrange("p u r -> p r u"))
+                    gx = gxp.tile([P, B, 4], BF16, name="gx", align_bytes=64)
+                    live["gx", a] = gx
+                gw = live["gx", a][:].rearrange("p r t -> p (r t)").bitcast(F32).rearrange("p (r u) -> p r u", u=2)
+                nc.scalar.copy(out=gw[:, bp * 256:(bp + 1) * 256, :],
+                               in_=live.pop(("xt", i, bp, g))[:].rearrange("p u r -> p r u"))
 
-        def x_quantise(a):
+        def xq(a):
             nc.vector.quantize_mx(
                 out=xc[:, a, :].bitcast(E5M2X4),
                 scales=xs[:, a, :],
-                in_=gx_of.pop(a)[:].rearrange("p r t -> p (r t)"),
+                in_=live.pop(("gx", a))[:].rearrange("p r t -> p (r t)"),
             )
 
-        def load_cn(half):
-            cols = slice(half * HALF, (half + 1) * HALF)
-            nc.sync.dma_start(out=c_sb[:, :, cols], in_=c_view[:, :, cols])
-            nc.sync.dma_start(out=n_sb[:, :, cols], in_=n_view[:, :, cols])
-
-        def halve_n(half):
+        def halve(half):
             cols = slice(half * HALF, (half + 1) * HALF)
             nc.vector.tensor_scalar_mul(out=n_sb[:, :, cols], in0=n_sb[:, :, cols], scalar1=0.5)
 
-        def where(e):
-            s = e // 4
-            return s // 2, (s % 2) * 4 + e % 4
-
-        def mx(e):
-            cod, scl = cod_of[e // 4]
-            cl = slice((e % 4) * P, (e % 4 + 1) * P)
-            acc = mxp.tile([P, B], F32, name="acc")
-            for a in range(4):
+        def mx(u):
+            s, a = divmod(u, 4)
+            cod, scl = live["cod", s]
+            for k in range(4):
+                e = 4 * s + k
+                if a == 0:
+                    acc = mxp.tile([P, B], F32, name="acc")
+                    live["acc", e] = acc
+                cl = slice(k * P, (k + 1) * P)
                 nc.tensor.matmul_mx(
-                    out=acc[:],
+                    out=live["acc", e][:],
                     lhsT=cod[:, a, cl].bitcast(E5M2X4),
                     lhsT_scale=scl[:, a, cl],
                     rhs=xc[:, a, :].bitcast(E5M2X4),
@@ -176,139 +225,226 @@ def tile_slstmcell_kernel(tc, x_t, h_prev, c_prev, n_prev, W, R, b, out_0, out_1
                     start=(a == 0),
                     stop=(a == 3),
                 )
-            acc_of[e] = acc
 
         def act(e):
-            q, ct = where(e)
-            acc = acc_of.pop(e)
-            if q == G_I:
+            gate, ct = where(e)
+            acc = live.pop(("acc", e))
+            if gate == G_I:
                 nc.scalar.activation(out=e_all[:, ct, :], in_=acc[:], func=AF.Exp,
                                      bias=bias[:, 8 + ct:9 + ct], scale=1.0)
                 return
             g = gp.tile([P, B], F32, name="g")
-            if q == G_Z:
+            if gate == G_Z:
                 nc.scalar.activation(out=g[:], in_=acc[:], func=AF.Tanh, bias=bias[:, ct:ct + 1], scale=1.0)
             else:
-                col = ct if q == G_F else 8 + ct
+                col = ct if gate == G_F else 8 + ct
                 nc.scalar.activation(out=g[:], in_=acc[:], func=AF.Tanh, bias=bhalf[:, col:col + 1], scale=0.5)
-            g_of[e] = g
+            live["g", e] = g
 
         def mid(e):
-            q, ct = where(e)
+            gate, ct = where(e)
             iz = izp.tile([P, B], F32, name="iz")
-            nc.vector.scalar_tensor_tensor(out=iz[:], in0=e_all[:, ct, :], scalar=50.0, in1=g_of.pop(e)[:],
+            nc.vector.scalar_tensor_tensor(out=iz[:], in0=e_all[:, ct, :], scalar=50.0, in1=live.pop(("g", e))[:],
                                            op0=ALU.min, op1=ALU.mult)
-            g_of[e] = iz
+            live["g", e] = iz
 
         def tr(e):
-            q, ct = where(e)
-            src = e_all[:, ct, :] if q == G_I else g_of.pop(e)[:]
+            gate, ct = where(e)
+            src = e_all[:, ct, :] if gate == G_I else live.pop(("g", e))[:]
             tp = tpp.tile([P, NBT, P], F32, name="tp")
             for bt in range(NBT):
                 nc.tensor.transpose(tp[:, bt, :], src[:, bt * P:(bt + 1) * P], ident[:])
-            tp_of[e] = tp
+            live["tp", e] = tp
 
         def fin(e):
-            q, ct = where(e)
+            gate, ct = where(e)
             cs = slice(ct * P, (ct + 1) * P)
-            tp = tp_of.pop(e)
-            if q == G_F:
-                nc.vector.scalar_tensor_tensor(out=fc[:, :, cs], in0=tp[:], scalar=1.0, in1=c_sb[:, :, cs],
-                                               op0=ALU.add, op1=ALU.mult)
-                nc.vector.scalar_tensor_tensor(out=fn[:, :, cs], in0=tp[:], scalar=1.0, in1=n_sb[:, :, cs],
-                                               op0=ALU.add, op1=ALU.mult)
-            elif q == G_I:
-                nc.vector.scalar_tensor_tensor(out=fn[:, :, cs], in0=tp[:], scalar=50.0, in1=fn[:, :, cs],
-                                               op0=ALU.min, op1=ALU.add)
-            elif q == G_Z:
-                nc.vector.scalar_tensor_tensor(out=fc[:, :, cs], in0=fc[:, :, cs], scalar=0.5, in1=tp[:],
-                                               op0=ALU.mult, op1=ALU.add)
+            tp = live.pop(("tp", e))
+            stt = nc.vector.scalar_tensor_tensor
+            if gate == G_F:
+                stt(out=fc[:, :, cs], in0=tp[:], scalar=1.0, in1=c_sb[:, :, cs], op0=ALU.add, op1=ALU.mult)
+                stt(out=fn[:, :, cs], in0=tp[:], scalar=1.0, in1=n_sb[:, :, cs], op0=ALU.add, op1=ALU.mult)
+            elif gate == G_I:
+                stt(out=fn[:, :, cs], in0=tp[:], scalar=50.0, in1=fn[:, :, cs], op0=ALU.min, op1=ALU.add)
+            elif gate == G_Z:
+                stt(out=fc[:, :, cs], in0=fc[:, :, cs], scalar=0.5, in1=tp[:], op0=ALU.mult, op1=ALU.add)
             else:
                 pair, lo = divmod(ct, 2)
                 if lo == 0:
                     hs = hsp.tile([P, NBT, 2 * P], F32, name="hs")
-                    hs_of[pair] = hs
-                hs = hs_of[pair]
-                nc.vector.scalar_tensor_tensor(out=hs[:, :, lo * P:(lo + 1) * P], in0=tp[:], scalar=1.0,
-                                               in1=fc[:, :, cs], op0=ALU.add, op1=ALU.mult)
-                if lo == 1:
-                    pc = slice(pair * 2 * P, (pair + 1) * 2 * P)
-                    nc.vector.scalar_tensor_tensor(out=hs[:], in0=hs[:], scalar=0.5, in1=rr[:, :, pc],
-                                                   op0=ALU.mult, op1=ALU.mult)
-                    nc.sync.dma_start(out=out_views[0][:, :, pc], in_=hs[:])
-            if q in (G_I, G_Z) and ct % 4 == 3:
-                hc = slice((ct // 4) * HALF, (ct // 4 + 1) * HALF)
-                if q == G_I:
-                    nc.sync.dma_start(out=out_views[2][:, :, hc], in_=fn[:, :, hc])
+                    live["hs", pair] = hs
+                hs = live["hs", pair]
+                stt(out=hs[:, :, lo * P:(lo + 1) * P], in0=tp[:], scalar=1.0, in1=rr[:, :, cs],
+                    op0=ALU.add, op1=ALU.mult)
+
+        def cr(half):
+            hc = slice(half * HALF, (half + 1) * HALF)
+            nc.vector.scalar_tensor_tensor(out=rr[:, :, hc], in0=fc[:, :, hc], scalar=0.5, in1=rr[:, :, hc],
+                                           op0=ALU.mult, op1=ALU.mult)
+
+        def ln(k):
+            nc.scalar.activation(out=rr[:, 2 * k:2 * k + 2, :], in_=fn[:, 2 * k:2 * k + 2, :], func=AF.Ln,
+                                 bias=1e-6, scale=1.0)
+
+        def ex(k):
+            nc.scalar.activation(out=rr[:, 2 * k:2 * k + 2, :], in_=rr[:, 2 * k:2 * k + 2, :], func=AF.Exp,
+                                 scale=-1.0)
+
+        emitters = {"ld": ld, "ldx": ldx, "ldcn": ldcn, "stn": stn, "stc": stc, "sth": sth, "ilv": ilv, "ils": ils,
+                    "q": q, "pil": pil, "pev": pev, "setup": setup, "bT": bT, "bcol": bcol, "xT": xT, "xev": xev, "xq": xq, "halve": halve,
+                    "cr": cr, "mx": mx, "act": act, "mid": mid, "tr": tr, "fin": fin, "ln": ln, "ex": ex}
+
+        sp = [("setup",), ("ld", 0), ("ldx", 0, 0), ("ldx", 0, 1), ("ld", 1), ("ldx", 1, 0), ("ldx", 1, 1),
+              ("ld", 2), ("ld", 3), ("ldcn", 0)]
+        sp += [("ld", u) for u in range(4, CN1_AT)] + [("ldcn", 1)] + [("ld", u) for u in range(CN1_AT, 32)]
+        sp += [("stn", 0), ("stn", 1), ("stc", 0), ("stc", 1)] + [("sth", p) for p in range(4)]
+
+        slots = range(-LEAD - SLEAD, 32)
+        pe = [("xT", 0, 0), ("xT", 0, 1), ("bT",), ("xT", 1, 0), ("xT", 1, 1)]
+        sc = [("xev", 0, 0), ("xev", 0, 1), ("xev", 1, 0), ("xev", 1, 1)]
+        ve = []
+        for j in slots:
+            u = j + LEAD
+            if 0 <= j + 1 < 32:
+                pe.append(("tr", j + 1))
+            if 0 <= u - 1 < 32:
+                pe.append(("mx", u - 1))
+            if u + SLEAD in PE_UNITS:
+                pe.append(("pil", u + SLEAD))
+            if j % 4 == 3 and 0 <= j + 1 < 32:
+                sc += [("act", j + 1 + k) for k in range(4)]
+            if 0 <= u + SLEAD < 32:
+                if u + SLEAD in PE_UNITS:
+                    sc.append(("pev", u + SLEAD))
+                elif V_COLS[u + SLEAD] < HALF:
+                    sc.append(("ils", u + SLEAD))
+            if j == LN_SLOT:
+                sc += [("ln", 0), ("ln", 1), ("ex", 0), ("ex", 1)]
+            if j >= 0:
+                ve.append(("fin", j))
+            if 0 <= j + ML < 32 and where(j + ML)[0] == G_Z:
+                ve.append(("mid", j + ML))
+            if j in CR_SLOTS:
+                ve.append(("cr", CR_SLOTS.index(j)))
+            if 0 <= u - 1 < 32:
+                ve.append(("q", u - 1))
+                if u - 1 < 2:
+                    ve += [("xq", 2 * (u - 1)), ("xq", 2 * (u - 1) + 1)]
+                if u - 1 == 0:
+                    ve.append(("bcol",))
+                if u - 1 == 3:
+                    ve.append(("halve", 0))
+                if u - 1 == 7:
+                    ve.append(("halve", 1))
+            if 0 <= u < 32 and V_COLS[u] > 0 and u not in PE_UNITS:
+                ve.append(("ilv", u))
+        queues = [sp, pe, sc, ve]
+        known = set()
+        for queue in queues:
+            known.update(queue)
+
+        def ring(pairs, bufs):
+            out = {}
+            for n, (taker, freer) in enumerate(pairs):
+                if n >= bufs:
+                    out.setdefault(taker, []).append(pairs[n - bufs][1])
+            return out
+
+        rings = []
+        tp_pairs = []
+        for k in pe:
+            if k[0] == "bT":
+                tp_pairs.append((k, ("bcol",)))
+            elif k[0] == "xT":
+                tp_pairs += [(k, ("xev",) + k[1:])] * 2
+            elif k[0] == "tr":
+                tp_pairs.append((k, ("fin", k[1])))
+            elif k[0] == "pil":
+                tp_pairs += [(k, ("pev", k[1]))] * 2
+        rings.append(ring(tp_pairs, 4))
+        rings.append(ring([(("mx", 4 * s), ("act", 4 * s + 3)) for s in range(8)], 1))
+        rings.append(ring([(k, (("mid" if where(k[1])[0] == G_Z else "tr"), k[1])) for k in sc
+                           if k[0] == "act" and where(k[1])[0] != G_I], G_BUFS))
+        rings.append(ring([(k, ("tr", k[1])) for k in ve if k[0] == "mid"], IZ_BUFS))
+        rings.append(ring([(("fin", 24 + 2 * p), ("sth", p)) for p in range(4)], 2))
+        rings.append(ring([(("ld", u), ("q", u)) for u in range(32)], RAW_BUFS))
+        rings.append(ring([(("ilv", u), ("q", u)) for u in range(32)], GRP_BUFS))
+        rings.append(ring([(("ils", u), ("q", u)) for u in range(32)], GRP_BUFS))
+        rings.append(ring([(("pev", u), ("q", u)) for u in range(32)], GRP_BUFS))
+        rings.append(ring([(("q", 4 * s), ("mx", 4 * s + 3)) for s in range(8)], COD_BUFS))
+        rings.append(ring([(("xev", i, 0), ("xq", 2 * i + 1)) for i in range(2)], 1))
+
+        def needs(key):
+            kind = key[0]
+            out = []
+            for r in rings:
+                out += r.get(key, [])
+            if kind != "setup":
+                out.append(("setup",))
+            if kind in ("ilv", "ils", "pil"):
+                out.append(("ld", key[1]))
+            elif kind == "pev":
+                out.append(("pil", key[1]))
+            elif kind == "q":
+                out += [("ilv", key[1]), ("ils", key[1]), ("pev", key[1])]
+            elif kind == "bcol":
+                out.append(("bT",))
+            elif kind == "xT":
+                out.append(("ldx",) + key[1:])
+            elif kind == "xev":
+                out.append(("xT",) + key[1:])
+            elif kind == "xq":
+                out += [("xev", key[1] // 2, 0), ("xev", key[1] // 2, 1)]
+            elif kind == "halve":
+                out.append(("ldcn", key[1]))
+            elif kind == "mx":
+                out += [("q", key[1]), ("xq", key[1] % 4)]
+                if key[1] % 4:
+                    out.append(("mx", key[1] - 1))
+            elif kind == "act":
+                out += [("mx", 4 * (key[1] // 4) + 3), ("bcol",)]
+            elif kind == "mid":
+                out += [("act", key[1]), ("act", key[1] - 8)]
+            elif kind == "tr":
+                out.append((("mid" if where(key[1])[0] == G_Z else "act"), key[1]))
+            elif kind == "fin":
+                e = key[1]
+                out.append(("tr", e))
+                gate, ct = where(e)
+                if gate == G_F:
+                    out.append(("halve", ct // 4))
+                elif gate == G_I:
+                    out.append(("fin", e - 8))
+                elif gate == G_Z:
+                    out.append(("fin", e - 16))
                 else:
-                    nc.sync.dma_start(out=out_views[1][:, :, hc], in_=fc[:, :, hc])
+                    out.append(("cr", ct // 4))
+                    if ct % 2 == 1:
+                        out.append(("fin", e - 1))
+            elif kind == "cr":
+                out += [("fin", 16 + 4 * key[1] + k) for k in range(4)] + [("ex", 0), ("ex", 1)]
+            elif kind == "ln":
+                out += [("fin", e) for e in range(8, 16)]
+            elif kind == "ex":
+                out.append(("ln", key[1]))
+            elif kind == "stn":
+                out += [("fin", 8 + 4 * key[1] + k) for k in range(4)]
+            elif kind == "stc":
+                out += [("fin", 16 + 4 * key[1] + k) for k in range(4)]
+            elif kind == "sth":
+                out.append(("fin", 24 + 2 * key[1] + 1))
+            return [k for k in out if k in known]
 
-        def reciprocal_of_n():
-            for k in range(2):
-                nc.scalar.activation(out=rr[:, 2 * k:2 * k + 2, :], in_=fn[:, 2 * k:2 * k + 2, :], func=AF.Ln,
-                                     bias=1e-6, scale=1.0)
-            for k in range(2):
-                nc.scalar.activation(out=rr[:, 2 * k:2 * k + 2, :], in_=rr[:, 2 * k:2 * k + 2, :], func=AF.Exp,
-                                     scale=-1.0)
-
-        load_unit(0)
-        load_x(0, 0)
-        load_x(0, 1)
-        load_unit(1)
-        load_x(1, 0)
-        load_x(1, 1)
-        load_unit(2)
-        load_unit(3)
-        load_cn(0)
-        for u in range(4, RAW_BUFS):
-            load_unit(u)
-        load_cn(1)
-
-        bps = tpp.tile([P, P], BF16, name="bps", tag="tp")
-        nc.tensor.transpose(bps[:], brow[:], identb[:])
-        nc.vector.tensor_copy(out=bias[:], in_=bps[:, 0:32])
-        nc.vector.tensor_scalar_mul(out=bhalf[:], in0=bps[:, 16:32], scalar1=0.5)
-
-        def shifted(e):
-            return BL if e >= EB else 0
-
-        def items(r, base, only_z=None):
-            found = []
-            for e in range(32):
-                z = where(e)[0] == G_Z
-                extra = 1 if (z and only_z is False) else 0
-                if only_z is True and not z:
-                    continue
-                if e + base + extra + shifted(e) == r:
-                    found.append(e)
-            return found
-
-        last_round = 31 + R_FIN + 1 + BL
-        for r in range(last_round + 1):
-            for e in items(r, R_ACT):
-                act(e)
-            if r == R_LN:
-                reciprocal_of_n()
-            if r < 4:
-                x_transpose(r // 2, r % 2)
-            for e in items(r, R_TR, False):
-                tr(e)
-            for e in items(r, R_MX):
-                mx(e)
-            if r in (1, 3):
-                x_quantise(r - 1)
-                x_quantise(r)
-            if r < 32:
-                interleave(r)
-                if r + RAW_BUFS < 32:
-                    load_unit(r + RAW_BUFS)
-            if r == 5:
-                halve_n(0)
-            if r == 9:
-                halve_n(1)
-            for e in items(r, R_MID, True):
-                mid(e)
-            for e in items(r, R_FIN, False):
-                fin(e)
-            if 1 <= r <= 32:
-                quantise(r - 1)
+        done = set()
+        heads = [0] * len(queues)
+        moved = True
+        while moved:
+            moved = False
+            for n, queue in enumerate(queues):
+                while heads[n] < len(queue) and all(k in done for k in needs(queue[heads[n]])):
+                    key = queue[heads[n]]
+                    emitters[key[0]](*key[1:])
+                    done.add(key)
+                    heads[n] += 1
+                    moved = True
+        assert all(heads[n] == len(queue) for n, queue in enumerate(queues))

@@ -17,27 +17,27 @@ FLOPS = 2 * B * (D + H) * 4 * H
 P = 128
 NBT = B // P
 HALF = 512
-GATE_ORDER = (2, 1, 0, 3)
+N_UNITS = 32
+N_ITEMS = 32
+GATE_COLUMN_BLOCK = (2, 1, 0, 3)
 G_F, G_I, G_Z, G_O = 0, 1, 2, 3
 
-MANUAL = False
 RAW_BUFS = 8
 GRP_BUFS = 5
 COD_BUFS = 3
 G_BUFS = 6
 IZ_BUFS = 3
-V_COLS = (512,512,512,512,128,128,96,96,96,96,96,96,96,96,160,160,160,160,160,160,160,160,96,512,512,512,512,96,96,96,96,96)
-PE_UNITS = (4, 6, 8, 10, 12, 14, 16, 18, 20, 22, 27, 29)
+V_COLS = (512,) * 6 + (144,) * 8 + (256,) * 8 + (128,) + (512,) * 5 + (0,) * 4
 LEAD = 6
-SLEAD = 1
-ML = 1
 CN1_AT = 10
-CR_SLOTS = (22, 26)
+CR_SLOTS = (23, 27)
 LN_SLOT = 15
+EX_SLOT = 19
 
 
 def tile_slstmcell_kernel(tc, x_t, h_prev, c_prev, n_prev, W, R, b, out_0, out_1, out_2):
     nc = tc.nc
+    stt = nc.vector.scalar_tensor_tensor
     with ExitStack() as ctx:
         const = ctx.enter_context(tc.tile_pool(name="const", bufs=1))
         keep = ctx.enter_context(tc.tile_pool(name="keep", bufs=1))
@@ -51,8 +51,7 @@ def tile_slstmcell_kernel(tc, x_t, h_prev, c_prev, n_prev, W, R, b, out_0, out_1
         hsp = ctx.enter_context(tc.tile_pool(name="hsp", bufs=2))
         mxp = ctx.enter_context(tc.psum_pool(name="mxp", bufs=4))
         tpp = ctx.enter_context(tc.psum_pool(name="tpp", bufs=4))
-        if MANUAL:
-            ctx.enter_context(tc.manual_schedule())
+        ctx.enter_context(tc.manual_schedule())
 
         warm = const.tile([P, 1], F32, name="warm")
         ident = const.tile([P, P], F32, name="ident")
@@ -71,7 +70,7 @@ def tile_slstmcell_kernel(tc, x_t, h_prev, c_prev, n_prev, W, R, b, out_0, out_1
 
         c_view = c_prev.rearrange("(p t) c -> p t c", t=NBT)
         n_view = n_prev.rearrange("(p t) c -> p t c", t=NBT)
-        out_views = [o.rearrange("(p t) c -> p t c", t=NBT) for o in (out_0, out_1, out_2)]
+        h_out, c_out, n_out = [o.rearrange("(p t) c -> p t c", t=NBT) for o in (out_0, out_1, out_2)]
 
         live = {}
 
@@ -79,9 +78,12 @@ def tile_slstmcell_kernel(tc, x_t, h_prev, c_prev, n_prev, W, R, b, out_0, out_1
             s = e // 4
             return s // 2, (s % 2) * 4 + e % 4
 
+        def half_cols(half):
+            return slice(half * HALF, (half + 1) * HALF)
+
         def ld(u):
             s, a = divmod(u, 4)
-            col0 = GATE_ORDER[s // 2] * H + (s % 2) * HALF
+            col0 = GATE_COLUMN_BLOCK[s // 2] * H + (s % 2) * HALF
             rows = (W if a < 2 else R)[(a % 2) * 512:(a % 2) * 512 + 512, col0:col0 + HALF]
             raw = rawp.tile([P, 4, HALF], BF16, name="raw")
             nc.sync.dma_start(out=raw[:], in_=rows.rearrange("(p j) w -> p j w", j=4))
@@ -95,21 +97,9 @@ def tile_slstmcell_kernel(tc, x_t, h_prev, c_prev, n_prev, W, R, b, out_0, out_1
             nc.sync.dma_start(out=live["xin", i][:, 2 * bp:2 * bp + 2, :], in_=view[:, 2 * bp:2 * bp + 2, :])
 
         def ldcn(half):
-            cols = slice(half * HALF, (half + 1) * HALF)
+            cols = half_cols(half)
             nc.sync.dma_start(out=c_sb[:, :, cols], in_=c_view[:, :, cols])
             nc.sync.dma_start(out=n_sb[:, :, cols], in_=n_view[:, :, cols])
-
-        def stn(half):
-            hc = slice(half * HALF, (half + 1) * HALF)
-            nc.sync.dma_start(out=out_views[2][:, :, hc], in_=fn[:, :, hc])
-
-        def stc(half):
-            hc = slice(half * HALF, (half + 1) * HALF)
-            nc.sync.dma_start(out=out_views[1][:, :, hc], in_=fc[:, :, hc])
-
-        def sth(pair):
-            pc = slice(pair * 2 * P, (pair + 1) * 2 * P)
-            nc.sync.dma_start(out=out_views[0][:, :, pc], in_=live.pop(("hs", pair))[:])
 
         def grp_tile(u):
             if ("grp", u) not in live:
@@ -117,29 +107,9 @@ def tile_slstmcell_kernel(tc, x_t, h_prev, c_prev, n_prev, W, R, b, out_0, out_1
                 live["grp", u] = grp
             return live["grp", u]
 
-        def ilv(u):
-            vc = V_COLS[u]
-            nc.vector.tensor_copy(out=grp_tile(u)[:, 0:vc, :].rearrange("p (c i) t -> p c t i", i=4),
-                                  in_=live["raw", u][:, :, 0:vc].rearrange("p t (c i) -> p c t i", i=4))
-
-        def ils(u):
-            vc = V_COLS[u]
-            nc.scalar.copy(out=grp_tile(u)[:, vc:HALF, :].rearrange("p (c i) t -> p c t i", i=4),
-                           in_=live["raw", u][:, :, vc:HALF].rearrange("p t (c i) -> p c t i", i=4))
-
-        def pil(u):
-            src = live["raw", u][:].rearrange("p j w -> p w j")
-            for k in range(2):
-                il = tpp.tile([P, 256, 4], BF16, name="il", tag="tp")
-                for m in range(2):
-                    w0 = 256 * k + 128 * m
-                    nc.tensor.matmul(out=il[:, 128 * m:128 * (m + 1), :], lhsT=identb[:], rhs=src[:, w0:w0 + 128, :],
-                                     start=True, stop=True)
-                live["il", u, k] = il
-
-        def pev(u):
-            for k in range(2):
-                nc.scalar.copy(out=grp_tile(u)[:, 256 * k:256 * (k + 1), :], in_=live.pop(("il", u, k))[:])
+        def interleave(copy, u, w0, w1):
+            copy(out=grp_tile(u)[:, w0:w1, :].rearrange("p (c i) t -> p c t i", i=4),
+                 in_=live["raw", u][:, :, w0:w1].rearrange("p t (c i) -> p c t i", i=4))
 
         def q(u):
             s, a = divmod(u, 4)
@@ -155,24 +125,6 @@ def tile_slstmcell_kernel(tc, x_t, h_prev, c_prev, n_prev, W, R, b, out_0, out_1
             )
             live.pop(("raw", u))
 
-        def setup():
-            nc.vector.memset(warm[:], 0.0)
-            nc.scalar.activation(out=warm[:], in_=warm[:], func=AF.Exp)
-            make_identity(nc, ident[:])
-            make_identity(nc, identb[:])
-            nc.gpsimd.memset(brow[:], 0.0)
-            nc.sync.dma_start(out=brow[0:32, :], in_=b.rearrange("(t c) -> t c", c=P))
-
-        def bT():
-            bps = tpp.tile([P, P], BF16, name="bps", tag="tp")
-            nc.tensor.transpose(bps[:], brow[:], identb[:])
-            live["bps"] = bps
-
-        def bcol():
-            bps = live.pop("bps")
-            nc.vector.tensor_copy(out=bias[:], in_=bps[:, 0:32])
-            nc.vector.tensor_scalar_mul(out=bhalf[:], in0=bps[:, 16:32], scalar1=0.5)
-
         def xT(i, bp):
             words = live["xin", i][:].bitcast(F32)
             for g in range(2):
@@ -184,17 +136,15 @@ def tile_slstmcell_kernel(tc, x_t, h_prev, c_prev, n_prev, W, R, b, out_0, out_1
                             words[:, 2 * bp + bl, 256 * g + u:256 * (g + 1):2],
                             ident[:],
                         )
-                live["xt", i, bp, g] = xt
-
-        def xev(i, bp):
-            for g in range(2):
                 a = 2 * i + g
                 if bp == 0:
                     gx = gxp.tile([P, B, 4], BF16, name="gx", align_bytes=64)
                     live["gx", a] = gx
                 gw = live["gx", a][:].rearrange("p r t -> p (r t)").bitcast(F32).rearrange("p (r u) -> p r u", u=2)
-                nc.scalar.copy(out=gw[:, bp * 256:(bp + 1) * 256, :],
-                               in_=live.pop(("xt", i, bp, g))[:].rearrange("p u r -> p r u"))
+                live["xt", g] = (xt, gw)
+            for g in range(2):
+                xt, gw = live.pop(("xt", g))
+                nc.scalar.copy(out=gw[:, bp * 256:(bp + 1) * 256, :], in_=xt[:].rearrange("p u r -> p r u"))
 
         def xq(a):
             nc.vector.quantize_mx(
@@ -204,7 +154,7 @@ def tile_slstmcell_kernel(tc, x_t, h_prev, c_prev, n_prev, W, R, b, out_0, out_1
             )
 
         def halve(half):
-            cols = slice(half * HALF, (half + 1) * HALF)
+            cols = half_cols(half)
             nc.vector.tensor_scalar_mul(out=n_sb[:, :, cols], in0=n_sb[:, :, cols], scalar1=0.5)
 
         def mx(u):
@@ -242,10 +192,9 @@ def tile_slstmcell_kernel(tc, x_t, h_prev, c_prev, n_prev, W, R, b, out_0, out_1
             live["g", e] = g
 
         def mid(e):
-            gate, ct = where(e)
+            ct = where(e)[1]
             iz = izp.tile([P, B], F32, name="iz")
-            nc.vector.scalar_tensor_tensor(out=iz[:], in0=e_all[:, ct, :], scalar=50.0, in1=live.pop(("g", e))[:],
-                                           op0=ALU.min, op1=ALU.mult)
+            stt(out=iz[:], in0=e_all[:, ct, :], scalar=50.0, in1=live.pop(("g", e))[:], op0=ALU.min, op1=ALU.mult)
             live["g", e] = iz
 
         def tr(e):
@@ -260,7 +209,6 @@ def tile_slstmcell_kernel(tc, x_t, h_prev, c_prev, n_prev, W, R, b, out_0, out_1
             gate, ct = where(e)
             cs = slice(ct * P, (ct + 1) * P)
             tp = live.pop(("tp", e))
-            stt = nc.vector.scalar_tensor_tensor
             if gate == G_F:
                 stt(out=fc[:, :, cs], in0=tp[:], scalar=1.0, in1=c_sb[:, :, cs], op0=ALU.add, op1=ALU.mult)
                 stt(out=fn[:, :, cs], in0=tp[:], scalar=1.0, in1=n_sb[:, :, cs], op0=ALU.add, op1=ALU.mult)
@@ -272,179 +220,84 @@ def tile_slstmcell_kernel(tc, x_t, h_prev, c_prev, n_prev, W, R, b, out_0, out_1
                 pair, lo = divmod(ct, 2)
                 if lo == 0:
                     hs = hsp.tile([P, NBT, 2 * P], F32, name="hs")
-                    live["hs", pair] = hs
-                hs = live["hs", pair]
-                stt(out=hs[:, :, lo * P:(lo + 1) * P], in0=tp[:], scalar=1.0, in1=rr[:, :, cs],
+                    live["hs"] = hs
+                stt(out=live["hs"][:, :, lo * P:(lo + 1) * P], in0=tp[:], scalar=1.0, in1=rr[:, :, cs],
                     op0=ALU.add, op1=ALU.mult)
+                if lo == 1:
+                    nc.sync.dma_start(out=h_out[:, :, pair * 2 * P:(pair + 1) * 2 * P], in_=live.pop("hs")[:])
 
         def cr(half):
-            hc = slice(half * HALF, (half + 1) * HALF)
-            nc.vector.scalar_tensor_tensor(out=rr[:, :, hc], in0=fc[:, :, hc], scalar=0.5, in1=rr[:, :, hc],
-                                           op0=ALU.mult, op1=ALU.mult)
+            hc = half_cols(half)
+            stt(out=rr[:, :, hc], in0=fc[:, :, hc], scalar=0.5, in1=rr[:, :, hc], op0=ALU.mult, op1=ALU.mult)
 
-        def ln(k):
-            nc.scalar.activation(out=rr[:, 2 * k:2 * k + 2, :], in_=fn[:, 2 * k:2 * k + 2, :], func=AF.Ln,
-                                 bias=1e-6, scale=1.0)
+        ld(0)
+        ldx(0, 0)
+        ldx(0, 1)
+        nc.vector.memset(warm[:], 0.0)
+        nc.scalar.activation(out=warm[:], in_=warm[:], func=AF.Exp)
+        nc.gpsimd.memset(brow[:], 0.0)
+        make_identity(nc, ident[:])
+        make_identity(nc, identb[:])
+        nc.sync.dma_start(out=brow[0:32, :], in_=b.rearrange("(t c) -> t c", c=P))
+        ld(1)
+        ldx(1, 0)
+        ldx(1, 1)
+        ld(2)
+        ld(3)
+        ldcn(0)
+        for u in range(4, RAW_BUFS):
+            ld(u)
+        xT(0, 0)
+        xT(0, 1)
+        bps = tpp.tile([P, P], BF16, name="bps", tag="tp")
+        nc.tensor.transpose(bps[:], brow[:], identb[:])
+        xT(1, 0)
+        xT(1, 1)
 
-        def ex(k):
-            nc.scalar.activation(out=rr[:, 2 * k:2 * k + 2, :], in_=rr[:, 2 * k:2 * k + 2, :], func=AF.Exp,
-                                 scale=-1.0)
-
-        emitters = {"ld": ld, "ldx": ldx, "ldcn": ldcn, "stn": stn, "stc": stc, "sth": sth, "ilv": ilv, "ils": ils,
-                    "q": q, "pil": pil, "pev": pev, "setup": setup, "bT": bT, "bcol": bcol, "xT": xT, "xev": xev, "xq": xq, "halve": halve,
-                    "cr": cr, "mx": mx, "act": act, "mid": mid, "tr": tr, "fin": fin, "ln": ln, "ex": ex}
-
-        sp = [("setup",), ("ld", 0), ("ldx", 0, 0), ("ldx", 0, 1), ("ld", 1), ("ldx", 1, 0), ("ldx", 1, 1),
-              ("ld", 2), ("ld", 3), ("ldcn", 0)]
-        sp += [("ld", u) for u in range(4, CN1_AT)] + [("ldcn", 1)] + [("ld", u) for u in range(CN1_AT, 32)]
-        sp += [("stn", 0), ("stn", 1), ("stc", 0), ("stc", 1)] + [("sth", p) for p in range(4)]
-
-        slots = range(-LEAD - SLEAD, 32)
-        pe = [("xT", 0, 0), ("xT", 0, 1), ("bT",), ("xT", 1, 0), ("xT", 1, 1)]
-        sc = [("xev", 0, 0), ("xev", 0, 1), ("xev", 1, 0), ("xev", 1, 1)]
-        ve = []
-        for j in slots:
+        for j in range(-LEAD - 1, N_ITEMS):
             u = j + LEAD
-            if 0 <= j + 1 < 32:
-                pe.append(("tr", j + 1))
-            if 0 <= u - 1 < 32:
-                pe.append(("mx", u - 1))
-            if u + SLEAD in PE_UNITS:
-                pe.append(("pil", u + SLEAD))
-            if j % 4 == 3 and 0 <= j + 1 < 32:
-                sc += [("act", j + 1 + k) for k in range(4)]
-            if 0 <= u + SLEAD < 32:
-                if u + SLEAD in PE_UNITS:
-                    sc.append(("pev", u + SLEAD))
-                elif V_COLS[u + SLEAD] < HALF:
-                    sc.append(("ils", u + SLEAD))
-            if j == LN_SLOT:
-                sc += [("ln", 0), ("ln", 1), ("ex", 0), ("ex", 1)]
+            if j % 4 == 3 and 0 <= j + 1 < N_ITEMS:
+                for e in range(j + 1, j + 5):
+                    act(e)
+            if 0 <= u + 1 < N_UNITS and V_COLS[u + 1] < HALF:
+                interleave(nc.scalar.copy, u + 1, V_COLS[u + 1], HALF)
             if j >= 0:
-                ve.append(("fin", j))
-            if 0 <= j + ML < 32 and where(j + ML)[0] == G_Z:
-                ve.append(("mid", j + ML))
+                fin(j)
+                if j in (19, 23):
+                    hc = half_cols((j - 19) // 4)
+                    nc.sync.dma_start(out=c_out[:, :, hc], in_=fc[:, :, hc])
+            if j == LN_SLOT:
+                for k in range(2):
+                    nc.scalar.activation(out=rr[:, 2 * k:2 * k + 2, :], in_=fn[:, 2 * k:2 * k + 2, :], func=AF.Ln,
+                                         bias=1e-6, scale=1.0)
+            if j == EX_SLOT:
+                for k in range(2):
+                    nc.scalar.activation(out=rr[:, 2 * k:2 * k + 2, :], in_=rr[:, 2 * k:2 * k + 2, :], func=AF.Exp,
+                                         scale=-1.0)
+            if 0 <= j + 1 < N_ITEMS and where(j + 1)[0] == G_Z:
+                mid(j + 1)
             if j in CR_SLOTS:
-                ve.append(("cr", CR_SLOTS.index(j)))
-            if 0 <= u - 1 < 32:
-                ve.append(("q", u - 1))
+                cr(CR_SLOTS.index(j))
+            if 0 <= j + 1 < N_ITEMS:
+                tr(j + 1)
+            if 0 <= u - 1 < N_UNITS:
+                q(u - 1)
                 if u - 1 < 2:
-                    ve += [("xq", 2 * (u - 1)), ("xq", 2 * (u - 1) + 1)]
+                    xq(2 * (u - 1))
+                    xq(2 * (u - 1) + 1)
                 if u - 1 == 0:
-                    ve.append(("bcol",))
-                if u - 1 == 3:
-                    ve.append(("halve", 0))
-                if u - 1 == 7:
-                    ve.append(("halve", 1))
-            if 0 <= u < 32 and V_COLS[u] > 0 and u not in PE_UNITS:
-                ve.append(("ilv", u))
-        queues = [sp, pe, sc, ve]
-        known = set()
-        for queue in queues:
-            known.update(queue)
-
-        def ring(pairs, bufs):
-            out = {}
-            for n, (taker, freer) in enumerate(pairs):
-                if n >= bufs:
-                    out.setdefault(taker, []).append(pairs[n - bufs][1])
-            return out
-
-        rings = []
-        tp_pairs = []
-        for k in pe:
-            if k[0] == "bT":
-                tp_pairs.append((k, ("bcol",)))
-            elif k[0] == "xT":
-                tp_pairs += [(k, ("xev",) + k[1:])] * 2
-            elif k[0] == "tr":
-                tp_pairs.append((k, ("fin", k[1])))
-            elif k[0] == "pil":
-                tp_pairs += [(k, ("pev", k[1]))] * 2
-        rings.append(ring(tp_pairs, 4))
-        rings.append(ring([(("mx", 4 * s), ("act", 4 * s + 3)) for s in range(8)], 1))
-        rings.append(ring([(k, (("mid" if where(k[1])[0] == G_Z else "tr"), k[1])) for k in sc
-                           if k[0] == "act" and where(k[1])[0] != G_I], G_BUFS))
-        rings.append(ring([(k, ("tr", k[1])) for k in ve if k[0] == "mid"], IZ_BUFS))
-        rings.append(ring([(("fin", 24 + 2 * p), ("sth", p)) for p in range(4)], 2))
-        rings.append(ring([(("ld", u), ("q", u)) for u in range(32)], RAW_BUFS))
-        rings.append(ring([(("ilv", u), ("q", u)) for u in range(32)], GRP_BUFS))
-        rings.append(ring([(("ils", u), ("q", u)) for u in range(32)], GRP_BUFS))
-        rings.append(ring([(("pev", u), ("q", u)) for u in range(32)], GRP_BUFS))
-        rings.append(ring([(("q", 4 * s), ("mx", 4 * s + 3)) for s in range(8)], COD_BUFS))
-        rings.append(ring([(("xev", i, 0), ("xq", 2 * i + 1)) for i in range(2)], 1))
-
-        def needs(key):
-            kind = key[0]
-            out = []
-            for r in rings:
-                out += r.get(key, [])
-            if kind != "setup":
-                out.append(("setup",))
-            if kind in ("ilv", "ils", "pil"):
-                out.append(("ld", key[1]))
-            elif kind == "pev":
-                out.append(("pil", key[1]))
-            elif kind == "q":
-                out += [("ilv", key[1]), ("ils", key[1]), ("pev", key[1])]
-            elif kind == "bcol":
-                out.append(("bT",))
-            elif kind == "xT":
-                out.append(("ldx",) + key[1:])
-            elif kind == "xev":
-                out.append(("xT",) + key[1:])
-            elif kind == "xq":
-                out += [("xev", key[1] // 2, 0), ("xev", key[1] // 2, 1)]
-            elif kind == "halve":
-                out.append(("ldcn", key[1]))
-            elif kind == "mx":
-                out += [("q", key[1]), ("xq", key[1] % 4)]
-                if key[1] % 4:
-                    out.append(("mx", key[1] - 1))
-            elif kind == "act":
-                out += [("mx", 4 * (key[1] // 4) + 3), ("bcol",)]
-            elif kind == "mid":
-                out += [("act", key[1]), ("act", key[1] - 8)]
-            elif kind == "tr":
-                out.append((("mid" if where(key[1])[0] == G_Z else "act"), key[1]))
-            elif kind == "fin":
-                e = key[1]
-                out.append(("tr", e))
-                gate, ct = where(e)
-                if gate == G_F:
-                    out.append(("halve", ct // 4))
-                elif gate == G_I:
-                    out.append(("fin", e - 8))
-                elif gate == G_Z:
-                    out.append(("fin", e - 16))
-                else:
-                    out.append(("cr", ct // 4))
-                    if ct % 2 == 1:
-                        out.append(("fin", e - 1))
-            elif kind == "cr":
-                out += [("fin", 16 + 4 * key[1] + k) for k in range(4)] + [("ex", 0), ("ex", 1)]
-            elif kind == "ln":
-                out += [("fin", e) for e in range(8, 16)]
-            elif kind == "ex":
-                out.append(("ln", key[1]))
-            elif kind == "stn":
-                out += [("fin", 8 + 4 * key[1] + k) for k in range(4)]
-            elif kind == "stc":
-                out += [("fin", 16 + 4 * key[1] + k) for k in range(4)]
-            elif kind == "sth":
-                out.append(("fin", 24 + 2 * key[1] + 1))
-            return [k for k in out if k in known]
-
-        done = set()
-        heads = [0] * len(queues)
-        moved = True
-        while moved:
-            moved = False
-            for n, queue in enumerate(queues):
-                while heads[n] < len(queue) and all(k in done for k in needs(queue[heads[n]])):
-                    key = queue[heads[n]]
-                    emitters[key[0]](*key[1:])
-                    done.add(key)
-                    heads[n] += 1
-                    moved = True
-        assert all(heads[n] == len(queue) for n, queue in enumerate(queues))
+                    nc.vector.tensor_copy(out=bias[:], in_=bps[:, 0:32])
+                    nc.vector.tensor_scalar_mul(out=bhalf[:], in0=bps[:, 16:32], scalar1=0.5)
+                if u - 1 in (3, 7):
+                    halve((u - 1) // 4)
+                nxt = u - 1 + RAW_BUFS
+                if nxt == CN1_AT:
+                    ldcn(1)
+                if nxt < N_UNITS:
+                    ld(nxt)
+                if nxt == N_UNITS - 1:
+                    for half in range(2):
+                        nc.sync.dma_start(out=n_out[:, :, half_cols(half)], in_=fn[:, :, half_cols(half)])
+                mx(u - 1)
+            if 0 <= u < N_UNITS and V_COLS[u] > 0:
+                interleave(nc.vector.tensor_copy, u, 0, V_COLS[u])

@@ -15,24 +15,30 @@ B, D, H = 512, 1024, 1024
 FLOPS = 2 * B * (D + H) * 4 * H
 
 P = 128
-NBT = B // P
-HALF = 512
-N_UNITS = 32
-N_ITEMS = 32
-GATE_COLUMN_BLOCK = (2, 1, 0, 3)
+PACK = 4
+K_PASS = P * PACK
+ROWS = B // P
+STEP = 512
+PASSES = (D + H) // K_PASS
+N_UNITS = 8 * PASSES
+N_ITEMS = 4 * H // P
 G_F, G_I, G_Z, G_O = 0, 1, 2, 3
+COLUMN_BLOCK = (2, 1, 0, 3)
+
+VECTOR_COLUMNS = (512,) * 6 + (144,) * 8 + (256,) * 10 + (512,) * 4 + (64,) * 4
+
+LEAD = 7
+TURN_LEAD = 2
+LN_SLOT = 15
+EXP_SLOT = 18
+SCALED_CELL_SLOTS = (23, 27)
+SECOND_STATE_LOAD_AT = 10
 
 RAW_BUFS = 8
-GRP_BUFS = 5
-COD_BUFS = 3
-G_BUFS = 6
-IZ_BUFS = 3
-V_COLS = (512,) * 6 + (144,) * 8 + (256,) * 8 + (128,) + (512,) * 5 + (0,) * 4
-LEAD = 6
-CN1_AT = 10
-CR_SLOTS = (23, 27)
-LN_SLOT = 15
-EX_SLOT = 19
+GROUPED_BUFS = 5
+CODE_BUFS = 3
+GATE_BUFS = 6
+PRODUCT_BUFS = 3
 
 
 def tile_slstmcell_kernel(tc, x_t, h_prev, c_prev, n_prev, W, R, b, out_0, out_1, out_2):
@@ -41,263 +47,270 @@ def tile_slstmcell_kernel(tc, x_t, h_prev, c_prev, n_prev, W, R, b, out_0, out_1
     with ExitStack() as ctx:
         const = ctx.enter_context(tc.tile_pool(name="const", bufs=1))
         keep = ctx.enter_context(tc.tile_pool(name="keep", bufs=1))
-        rawp = ctx.enter_context(tc.tile_pool(name="rawp", bufs=RAW_BUFS))
-        xinp = ctx.enter_context(tc.tile_pool(name="xinp", bufs=2))
-        gxp = ctx.enter_context(tc.tile_pool(name="gxp", bufs=2))
-        grpp = ctx.enter_context(tc.tile_pool(name="grpp", bufs=GRP_BUFS))
-        codp = ctx.enter_context(tc.tile_pool(name="codp", bufs=COD_BUFS))
-        gp = ctx.enter_context(tc.tile_pool(name="gp", bufs=G_BUFS))
-        izp = ctx.enter_context(tc.tile_pool(name="izp", bufs=IZ_BUFS))
-        hsp = ctx.enter_context(tc.tile_pool(name="hsp", bufs=2))
-        mxp = ctx.enter_context(tc.psum_pool(name="mxp", bufs=4))
-        tpp = ctx.enter_context(tc.psum_pool(name="tpp", bufs=4))
+        raw_pool = ctx.enter_context(tc.tile_pool(name="raw_pool", bufs=RAW_BUFS))
+        rows_pool = ctx.enter_context(tc.tile_pool(name="rows_pool", bufs=2))
+        rows_grouped_pool = ctx.enter_context(tc.tile_pool(name="rows_grouped_pool", bufs=2))
+        grouped_pool = ctx.enter_context(tc.tile_pool(name="grouped_pool", bufs=GROUPED_BUFS))
+        code_pool = ctx.enter_context(tc.tile_pool(name="code_pool", bufs=CODE_BUFS))
+        gate_pool = ctx.enter_context(tc.tile_pool(name="gate_pool", bufs=GATE_BUFS))
+        product_pool = ctx.enter_context(tc.tile_pool(name="product_pool", bufs=PRODUCT_BUFS))
+        h_pool = ctx.enter_context(tc.tile_pool(name="h_pool", bufs=2))
+        sum_pool = ctx.enter_context(tc.psum_pool(name="sum_pool", bufs=4))
+        turn_pool = ctx.enter_context(tc.psum_pool(name="turn_pool", bufs=4))
         ctx.enter_context(tc.manual_schedule())
 
-        warm = const.tile([P, 1], F32, name="warm")
-        ident = const.tile([P, P], F32, name="ident")
-        identb = const.tile([P, P], BF16, name="identb")
-        brow = const.tile([P, P], BF16, name="brow")
-        bias = const.tile([P, 32], F32, name="bias")
-        bhalf = const.tile([P, 16], F32, name="bhalf")
-        c_sb = keep.tile([P, NBT, H], BF16, name="c_sb")
-        n_sb = keep.tile([P, NBT, H], BF16, name="n_sb")
-        fc = keep.tile([P, NBT, H], F32, name="fc")
-        fn = keep.tile([P, NBT, H], F32, name="fn")
-        rr = keep.tile([P, NBT, H], F32, name="rr")
-        e_all = keep.tile([P, 8, B], F32, name="e_all")
-        xc = keep.tile([P, 4, B], U32, name="xc", align_bytes=64)
-        xs = keep.tile([P, 4, B], U8, name="xs", align_bytes=64)
+        table_warmer = const.tile([P, 1], F32, name="table_warmer")
+        ident_f32 = const.tile([P, P], F32, name="ident_f32")
+        ident_bf16 = const.tile([P, P], BF16, name="ident_bf16")
+        b_rows = const.tile([P, P], BF16, name="b_rows")
+        bias = const.tile([P, 4 * H // P], F32, name="bias")
+        bias_half = const.tile([P, 2 * H // P], F32, name="bias_half")
+        c_sb = keep.tile([P, ROWS, H], BF16, name="c_sb")
+        n_half = keep.tile([P, ROWS, H], BF16, name="n_half")
+        cell = keep.tile([P, ROWS, H], F32, name="cell")
+        norm = keep.tile([P, ROWS, H], F32, name="norm")
+        ratio = keep.tile([P, ROWS, H], F32, name="ratio")
+        exp_i = keep.tile([P, H // P, B], F32, name="exp_i")
+        x_codes = keep.tile([P, PASSES, B], U32, name="x_codes", align_bytes=64)
+        x_scales = keep.tile([P, PASSES, B], U8, name="x_scales", align_bytes=64)
 
-        c_view = c_prev.rearrange("(p t) c -> p t c", t=NBT)
-        n_view = n_prev.rearrange("(p t) c -> p t c", t=NBT)
-        h_out, c_out, n_out = [o.rearrange("(p t) c -> p t c", t=NBT) for o in (out_0, out_1, out_2)]
+        c_view = c_prev.rearrange("(p t) c -> p t c", t=ROWS)
+        n_view = n_prev.rearrange("(p t) c -> p t c", t=ROWS)
+        h_out, c_out, n_out = [o.rearrange("(p t) c -> p t c", t=ROWS) for o in (out_0, out_1, out_2)]
 
         live = {}
 
-        def where(e):
+        def gate_and_tile(e):
             s = e // 4
             return s // 2, (s % 2) * 4 + e % 4
 
-        def half_cols(half):
-            return slice(half * HALF, (half + 1) * HALF)
+        def half_columns(half):
+            return slice(half * STEP, (half + 1) * STEP)
 
-        def ld(u):
-            s, a = divmod(u, 4)
-            col0 = GATE_COLUMN_BLOCK[s // 2] * H + (s % 2) * HALF
-            rows = (W if a < 2 else R)[(a % 2) * 512:(a % 2) * 512 + 512, col0:col0 + HALF]
-            raw = rawp.tile([P, 4, HALF], BF16, name="raw")
-            nc.sync.dma_start(out=raw[:], in_=rows.rearrange("(p j) w -> p j w", j=4))
+        def load_unit(u):
+            s, a = divmod(u, PASSES)
+            col0 = COLUMN_BLOCK[s // 2] * H + (s % 2) * STEP
+            row0 = (a % 2) * K_PASS
+            rows = (W if a < 2 else R)[row0:row0 + K_PASS, col0:col0 + STEP]
+            raw = raw_pool.tile([P, PACK, STEP], BF16, name="raw")
+            nc.sync.dma_start(out=raw[:], in_=rows.rearrange("(p t) w -> p t w", t=PACK))
             live["raw", u] = raw
 
-        def ldx(i, bp):
-            if bp == 0:
-                xin = xinp.tile([P, NBT, D], BF16, name="xin")
-                live["xin", i] = xin
-            view = (x_t, h_prev)[i].rearrange("(p t) k -> p t k", t=NBT)
-            nc.sync.dma_start(out=live["xin", i][:, 2 * bp:2 * bp + 2, :], in_=view[:, 2 * bp:2 * bp + 2, :])
-
-        def ldcn(half):
-            cols = half_cols(half)
-            nc.sync.dma_start(out=c_sb[:, :, cols], in_=c_view[:, :, cols])
-            nc.sync.dma_start(out=n_sb[:, :, cols], in_=n_view[:, :, cols])
-
-        def grp_tile(u):
-            if ("grp", u) not in live:
-                grp = grpp.tile([P, HALF, 4], BF16, name="grp", align_bytes=64)
-                live["grp", u] = grp
-            return live["grp", u]
-
         def interleave(copy, u, w0, w1):
-            copy(out=grp_tile(u)[:, w0:w1, :].rearrange("p (c i) t -> p c t i", i=4),
+            if ("grouped", u) not in live:
+                grouped = grouped_pool.tile([P, STEP, PACK], BF16, name="grouped", align_bytes=64)
+                live["grouped", u] = grouped
+            copy(out=live["grouped", u][:, w0:w1, :].rearrange("p (c i) t -> p c t i", i=4),
                  in_=live["raw", u][:, :, w0:w1].rearrange("p t (c i) -> p c t i", i=4))
 
-        def q(u):
-            s, a = divmod(u, 4)
+        def quantise_unit(u):
+            s, a = divmod(u, PASSES)
             if a == 0:
-                cod = codp.tile([P, 4, HALF], U32, name="cod", align_bytes=64)
-                scl = codp.tile([P, 4, HALF], U8, name="scl", align_bytes=64)
-                live["cod", s] = (cod, scl)
-            cod, scl = live["cod", s]
+                codes = code_pool.tile([P, PASSES, STEP], U32, name="codes", align_bytes=64)
+                scales = code_pool.tile([P, PASSES, STEP], U8, name="scales", align_bytes=64)
+                live["codes", s] = (codes, scales)
+            codes, scales = live["codes", s]
             nc.vector.quantize_mx(
-                out=cod[:, a, :].bitcast(E5M2X4),
-                scales=scl[:, a, :],
-                in_=live.pop(("grp", u))[:].rearrange("p w j -> p (w j)"),
+                out=codes[:, a, :].bitcast(E5M2X4),
+                scales=scales[:, a, :],
+                in_=live.pop(("grouped", u))[:].rearrange("p w t -> p (w t)"),
             )
             live.pop(("raw", u))
 
-        def xT(i, bp):
-            words = live["xin", i][:].bitcast(F32)
-            for g in range(2):
-                xt = tpp.tile([P, 2, 256], F32, name="xt", tag="tp")
-                for u in range(2):
-                    for bl in range(2):
-                        nc.tensor.transpose(
-                            xt[:, u, bl * P:(bl + 1) * P],
-                            words[:, 2 * bp + bl, 256 * g + u:256 * (g + 1):2],
-                            ident[:],
-                        )
-                a = 2 * i + g
-                if bp == 0:
-                    gx = gxp.tile([P, B, 4], BF16, name="gx", align_bytes=64)
-                    live["gx", a] = gx
-                gw = live["gx", a][:].rearrange("p r t -> p (r t)").bitcast(F32).rearrange("p (r u) -> p r u", u=2)
-                live["xt", g] = (xt, gw)
-            for g in range(2):
-                xt, gw = live.pop(("xt", g))
-                nc.scalar.copy(out=gw[:, bp * 256:(bp + 1) * 256, :], in_=xt[:].rearrange("p u r -> p r u"))
+        def load_rows(i, pair):
+            if pair == 0:
+                rows_in = rows_pool.tile([P, ROWS, D], BF16, name="rows_in")
+                live["rows_in", i] = rows_in
+            view = (x_t, h_prev)[i].rearrange("(p t) k -> p t k", t=ROWS)
+            nc.sync.dma_start(out=live["rows_in", i][:, 2 * pair:2 * pair + 2, :], in_=view[:, 2 * pair:2 * pair + 2, :])
 
-        def xq(a):
+        def transpose_rows(i, pair):
+            words = live["rows_in", i][:].bitcast(F32)
+            turned = []
+            for g in range(2):
+                turn = turn_pool.tile([P, 2, 2 * P], F32, name="turn")
+                for u in range(2):
+                    for r in range(2):
+                        nc.tensor.transpose(
+                            turn[:, u, r * P:(r + 1) * P],
+                            words[:, 2 * pair + r, 256 * g + u:256 * (g + 1):2],
+                            ident_f32[:],
+                        )
+                turned.append(turn)
+            for g in range(2):
+                a = 2 * i + g
+                if pair == 0:
+                    rows_grouped = rows_grouped_pool.tile([P, B, PACK], BF16, name="rows_grouped", align_bytes=64)
+                    live["rows_grouped", a] = rows_grouped
+                as_words = live["rows_grouped", a][:].rearrange("p r t -> p (r t)").bitcast(F32)
+                nc.scalar.copy(
+                    out=as_words.rearrange("p (r u) -> p r u", u=2)[:, pair * 2 * P:(pair + 1) * 2 * P, :],
+                    in_=turned[g][:].rearrange("p u r -> p r u"),
+                )
+
+        def quantise_rows(a):
             nc.vector.quantize_mx(
-                out=xc[:, a, :].bitcast(E5M2X4),
-                scales=xs[:, a, :],
-                in_=live.pop(("gx", a))[:].rearrange("p r t -> p (r t)"),
+                out=x_codes[:, a, :].bitcast(E5M2X4),
+                scales=x_scales[:, a, :],
+                in_=live.pop(("rows_grouped", a))[:].rearrange("p r t -> p (r t)"),
             )
 
-        def halve(half):
-            cols = half_cols(half)
-            nc.vector.tensor_scalar_mul(out=n_sb[:, :, cols], in0=n_sb[:, :, cols], scalar1=0.5)
+        def load_state(half):
+            cols = half_columns(half)
+            nc.sync.dma_start(out=c_sb[:, :, cols], in_=c_view[:, :, cols])
+            nc.sync.dma_start(out=n_half[:, :, cols], in_=n_view[:, :, cols])
 
-        def mx(u):
-            s, a = divmod(u, 4)
-            cod, scl = live["cod", s]
+        def halve_n(half):
+            cols = half_columns(half)
+            nc.vector.tensor_scalar_mul(out=n_half[:, :, cols], in0=n_half[:, :, cols], scalar1=0.5)
+
+        def multiply_pass(u):
+            s, a = divmod(u, PASSES)
+            codes, scales = live["codes", s]
             for k in range(4):
                 e = 4 * s + k
                 if a == 0:
-                    acc = mxp.tile([P, B], F32, name="acc")
-                    live["acc", e] = acc
-                cl = slice(k * P, (k + 1) * P)
+                    sums = sum_pool.tile([P, B], F32, name="sums")
+                    live["sums", e] = sums
+                channels = slice(k * P, (k + 1) * P)
                 nc.tensor.matmul_mx(
-                    out=live["acc", e][:],
-                    lhsT=cod[:, a, cl].bitcast(E5M2X4),
-                    lhsT_scale=scl[:, a, cl],
-                    rhs=xc[:, a, :].bitcast(E5M2X4),
-                    rhs_scale=xs[:, a, :],
+                    out=live["sums", e][:],
+                    lhsT=codes[:, a, channels].bitcast(E5M2X4),
+                    lhsT_scale=scales[:, a, channels],
+                    rhs=x_codes[:, a, :].bitcast(E5M2X4),
+                    rhs_scale=x_scales[:, a, :],
                     start=(a == 0),
-                    stop=(a == 3),
+                    stop=(a == PASSES - 1),
                 )
 
-        def act(e):
-            gate, ct = where(e)
-            acc = live.pop(("acc", e))
+        def gate_function(e):
+            gate, c = gate_and_tile(e)
+            sums = live.pop(("sums", e))
             if gate == G_I:
-                nc.scalar.activation(out=e_all[:, ct, :], in_=acc[:], func=AF.Exp,
-                                     bias=bias[:, 8 + ct:9 + ct], scale=1.0)
+                nc.scalar.activation(out=exp_i[:, c, :], in_=sums[:], func=AF.Exp,
+                                     bias=bias[:, 8 + c:9 + c], scale=1.0)
                 return
-            g = gp.tile([P, B], F32, name="g")
+            value = gate_pool.tile([P, B], F32, name="value")
             if gate == G_Z:
-                nc.scalar.activation(out=g[:], in_=acc[:], func=AF.Tanh, bias=bias[:, ct:ct + 1], scale=1.0)
+                nc.scalar.activation(out=value[:], in_=sums[:], func=AF.Tanh, bias=bias[:, c:c + 1], scale=1.0)
             else:
-                col = ct if gate == G_F else 8 + ct
-                nc.scalar.activation(out=g[:], in_=acc[:], func=AF.Tanh, bias=bhalf[:, col:col + 1], scale=0.5)
-            live["g", e] = g
+                col = c if gate == G_F else 8 + c
+                nc.scalar.activation(out=value[:], in_=sums[:], func=AF.Tanh, bias=bias_half[:, col:col + 1],
+                                     scale=0.5)
+            live["value", e] = value
 
-        def mid(e):
-            ct = where(e)[1]
-            iz = izp.tile([P, B], F32, name="iz")
-            stt(out=iz[:], in0=e_all[:, ct, :], scalar=50.0, in1=live.pop(("g", e))[:], op0=ALU.min, op1=ALU.mult)
-            live["g", e] = iz
+        def input_times_candidate(e):
+            c = gate_and_tile(e)[1]
+            product = product_pool.tile([P, B], F32, name="product")
+            stt(out=product[:], in0=exp_i[:, c, :], scalar=50.0, in1=live.pop(("value", e))[:],
+                op0=ALU.min, op1=ALU.mult)
+            live["value", e] = product
 
-        def tr(e):
-            gate, ct = where(e)
-            src = e_all[:, ct, :] if gate == G_I else live.pop(("g", e))[:]
-            tp = tpp.tile([P, NBT, P], F32, name="tp")
-            for bt in range(NBT):
-                nc.tensor.transpose(tp[:, bt, :], src[:, bt * P:(bt + 1) * P], ident[:])
-            live["tp", e] = tp
+        def turn_item(e):
+            gate, c = gate_and_tile(e)
+            src = exp_i[:, c, :] if gate == G_I else live.pop(("value", e))[:]
+            turn = turn_pool.tile([P, ROWS, P], F32, name="turn")
+            for t in range(ROWS):
+                nc.tensor.transpose(turn[:, t, :], src[:, t * P:(t + 1) * P], ident_f32[:])
+            live["turn", e] = turn
 
-        def fin(e):
-            gate, ct = where(e)
-            cs = slice(ct * P, (ct + 1) * P)
-            tp = live.pop(("tp", e))
+        def finish_item(e):
+            gate, c = gate_and_tile(e)
+            cols = slice(c * P, (c + 1) * P)
+            turn = live.pop(("turn", e))
             if gate == G_F:
-                stt(out=fc[:, :, cs], in0=tp[:], scalar=1.0, in1=c_sb[:, :, cs], op0=ALU.add, op1=ALU.mult)
-                stt(out=fn[:, :, cs], in0=tp[:], scalar=1.0, in1=n_sb[:, :, cs], op0=ALU.add, op1=ALU.mult)
+                stt(out=cell[:, :, cols], in0=turn[:], scalar=1.0, in1=c_sb[:, :, cols], op0=ALU.add, op1=ALU.mult)
+                stt(out=norm[:, :, cols], in0=turn[:], scalar=1.0, in1=n_half[:, :, cols], op0=ALU.add, op1=ALU.mult)
             elif gate == G_I:
-                stt(out=fn[:, :, cs], in0=tp[:], scalar=50.0, in1=fn[:, :, cs], op0=ALU.min, op1=ALU.add)
+                stt(out=norm[:, :, cols], in0=turn[:], scalar=50.0, in1=norm[:, :, cols], op0=ALU.min, op1=ALU.add)
             elif gate == G_Z:
-                stt(out=fc[:, :, cs], in0=fc[:, :, cs], scalar=0.5, in1=tp[:], op0=ALU.mult, op1=ALU.add)
+                stt(out=cell[:, :, cols], in0=cell[:, :, cols], scalar=0.5, in1=turn[:], op0=ALU.mult, op1=ALU.add)
             else:
-                pair, lo = divmod(ct, 2)
-                if lo == 0:
-                    hs = hsp.tile([P, NBT, 2 * P], F32, name="hs")
-                    live["hs"] = hs
-                stt(out=live["hs"][:, :, lo * P:(lo + 1) * P], in0=tp[:], scalar=1.0, in1=rr[:, :, cs],
-                    op0=ALU.add, op1=ALU.mult)
-                if lo == 1:
-                    nc.sync.dma_start(out=h_out[:, :, pair * 2 * P:(pair + 1) * 2 * P], in_=live.pop("hs")[:])
+                pair, second = divmod(c, 2)
+                if not second:
+                    h_tile = h_pool.tile([P, ROWS, 2 * P], F32, name="h_tile")
+                    live["h_tile"] = h_tile
+                stt(out=live["h_tile"][:, :, second * P:(second + 1) * P], in0=turn[:], scalar=1.0,
+                    in1=ratio[:, :, cols], op0=ALU.add, op1=ALU.mult)
+                if second:
+                    nc.sync.dma_start(out=h_out[:, :, pair * 2 * P:(pair + 1) * 2 * P], in_=live.pop("h_tile")[:])
 
-        def cr(half):
-            hc = half_cols(half)
-            stt(out=rr[:, :, hc], in0=fc[:, :, hc], scalar=0.5, in1=rr[:, :, hc], op0=ALU.mult, op1=ALU.mult)
+        def scaled_cell(half):
+            cols = half_columns(half)
+            stt(out=ratio[:, :, cols], in0=cell[:, :, cols], scalar=0.5, in1=ratio[:, :, cols],
+                op0=ALU.mult, op1=ALU.mult)
 
-        ld(0)
-        ldx(0, 0)
-        ldx(0, 1)
-        nc.vector.memset(warm[:], 0.0)
-        nc.scalar.activation(out=warm[:], in_=warm[:], func=AF.Exp)
-        nc.gpsimd.memset(brow[:], 0.0)
-        make_identity(nc, ident[:])
-        make_identity(nc, identb[:])
-        nc.sync.dma_start(out=brow[0:32, :], in_=b.rearrange("(t c) -> t c", c=P))
-        ld(1)
-        ldx(1, 0)
-        ldx(1, 1)
-        ld(2)
-        ld(3)
-        ldcn(0)
+        load_rows(0, 0)
+        load_rows(0, 1)
+        load_unit(0)
+        nc.vector.memset(table_warmer[:], 0.0)
+        nc.scalar.activation(out=table_warmer[:], in_=table_warmer[:], func=AF.Exp)
+        nc.gpsimd.memset(b_rows[:], 0.0)
+        make_identity(nc, ident_f32[:])
+        make_identity(nc, ident_bf16[:])
+        nc.sync.dma_start(out=b_rows[0:4 * H // P, :], in_=b.rearrange("(t c) -> t c", c=P))
+        load_rows(1, 0)
+        load_rows(1, 1)
+        load_unit(1)
+        load_unit(2)
+        load_unit(3)
+        load_state(0)
         for u in range(4, RAW_BUFS):
-            ld(u)
-        xT(0, 0)
-        xT(0, 1)
-        bps = tpp.tile([P, P], BF16, name="bps", tag="tp")
-        nc.tensor.transpose(bps[:], brow[:], identb[:])
-        xT(1, 0)
-        xT(1, 1)
+            load_unit(u)
+        transpose_rows(0, 0)
+        transpose_rows(0, 1)
+        b_turn = turn_pool.tile([P, P], BF16, name="b_turn", tag="turn")
+        nc.tensor.transpose(b_turn[:], b_rows[:], ident_bf16[:])
+        transpose_rows(1, 0)
+        transpose_rows(1, 1)
 
         for j in range(-LEAD - 1, N_ITEMS):
             u = j + LEAD
-            if j % 4 == 3 and 0 <= j + 1 < N_ITEMS:
-                for e in range(j + 1, j + 5):
-                    act(e)
-            if 0 <= u + 1 < N_UNITS and V_COLS[u + 1] < HALF:
-                interleave(nc.scalar.copy, u + 1, V_COLS[u + 1], HALF)
+            first = u - 5
+            if first % 4 == 0 and 0 <= first < N_ITEMS:
+                for e in range(first, first + 4):
+                    gate_function(e)
+            if 0 <= u + 1 < N_UNITS and VECTOR_COLUMNS[u + 1] < STEP:
+                interleave(nc.scalar.copy, u + 1, VECTOR_COLUMNS[u + 1], STEP)
             if j >= 0:
-                fin(j)
-                if j in (19, 23):
-                    hc = half_cols((j - 19) // 4)
-                    nc.sync.dma_start(out=c_out[:, :, hc], in_=fc[:, :, hc])
+                finish_item(j)
+                if gate_and_tile(j)[0] == G_Z and j % 4 == 3:
+                    cols = half_columns((j // 4) % 2)
+                    nc.sync.dma_start(out=c_out[:, :, cols], in_=cell[:, :, cols])
             if j == LN_SLOT:
                 for k in range(2):
-                    nc.scalar.activation(out=rr[:, 2 * k:2 * k + 2, :], in_=fn[:, 2 * k:2 * k + 2, :], func=AF.Ln,
+                    nc.scalar.activation(out=ratio[:, 2 * k:2 * k + 2, :], in_=norm[:, 2 * k:2 * k + 2, :], func=AF.Ln,
                                          bias=1e-6, scale=1.0)
-            if j == EX_SLOT:
+            if j == EXP_SLOT:
                 for k in range(2):
-                    nc.scalar.activation(out=rr[:, 2 * k:2 * k + 2, :], in_=rr[:, 2 * k:2 * k + 2, :], func=AF.Exp,
+                    nc.scalar.activation(out=ratio[:, 2 * k:2 * k + 2, :], in_=ratio[:, 2 * k:2 * k + 2, :], func=AF.Exp,
                                          scale=-1.0)
-            if 0 <= j + 1 < N_ITEMS and where(j + 1)[0] == G_Z:
-                mid(j + 1)
-            if j in CR_SLOTS:
-                cr(CR_SLOTS.index(j))
-            if 0 <= j + 1 < N_ITEMS:
-                tr(j + 1)
+            ahead = j + TURN_LEAD
+            if 0 <= ahead < N_ITEMS:
+                if gate_and_tile(ahead)[0] == G_Z:
+                    input_times_candidate(ahead)
+            if j in SCALED_CELL_SLOTS:
+                scaled_cell(SCALED_CELL_SLOTS.index(j))
+            if 0 <= ahead < N_ITEMS:
+                turn_item(ahead)
             if 0 <= u - 1 < N_UNITS:
-                q(u - 1)
+                quantise_unit(u - 1)
                 if u - 1 < 2:
-                    xq(2 * (u - 1))
-                    xq(2 * (u - 1) + 1)
+                    quantise_rows(2 * (u - 1))
+                    quantise_rows(2 * (u - 1) + 1)
                 if u - 1 == 0:
-                    nc.vector.tensor_copy(out=bias[:], in_=bps[:, 0:32])
-                    nc.vector.tensor_scalar_mul(out=bhalf[:], in0=bps[:, 16:32], scalar1=0.5)
+                    nc.vector.tensor_copy(out=bias[:], in_=b_turn[:, 0:32])
+                    nc.vector.tensor_scalar_mul(out=bias_half[:], in0=b_turn[:, 16:32], scalar1=0.5)
                 if u - 1 in (3, 7):
-                    halve((u - 1) // 4)
-                nxt = u - 1 + RAW_BUFS
-                if nxt == CN1_AT:
-                    ldcn(1)
-                if nxt < N_UNITS:
-                    ld(nxt)
-                if nxt == N_UNITS - 1:
+                    halve_n((u - 1) // 4)
+                following = u - 1 + RAW_BUFS
+                if following == SECOND_STATE_LOAD_AT:
+                    load_state(1)
+                if following < N_UNITS:
+                    load_unit(following)
+                if following == N_UNITS - 1:
                     for half in range(2):
-                        nc.sync.dma_start(out=n_out[:, :, half_cols(half)], in_=fn[:, :, half_cols(half)])
-                mx(u - 1)
-            if 0 <= u < N_UNITS and V_COLS[u] > 0:
-                interleave(nc.vector.tensor_copy, u, 0, V_COLS[u])
+                        nc.sync.dma_start(out=n_out[:, :, half_columns(half)], in_=norm[:, :, half_columns(half)])
+                multiply_pass(u - 1)
+            if 0 <= u < N_UNITS and VECTOR_COLUMNS[u] > 0:
+                interleave(nc.vector.tensor_copy, u, 0, VECTOR_COLUMNS[u])

@@ -25,7 +25,10 @@ N_ITEMS = 4 * H // P
 G_F, G_I, G_Z, G_O = 0, 1, 2, 3
 COLUMN_BLOCK = (2, 1, 0, 3)
 
-VECTOR_COLUMNS = (512,) * 6 + (144,) * 8 + (256,) * 10 + (512,) * 4 + (64,) * 4
+VECTOR_COLUMNS = (512,) * 6 + (144,) * 2 + (32, 64) * 4 + (208, 240) * 4 + (384, 512) * 2 + (64, 64) * 2
+
+GPSIMD_COLUMNS = (0,) * 8 + (352, 0) * 4 + (128, 0) * 8
+GPSIMD_LEAD = 8
 
 LEAD = 7
 TURN_LEAD = 2
@@ -60,6 +63,7 @@ def tile_slstmcell_kernel(tc, x_t, h_prev, c_prev, n_prev, W, R, b, out_0, out_1
         ctx.enter_context(tc.manual_schedule())
 
         table_warmer = const.tile([P, 1], F32, name="table_warmer")
+        baton = const.tile([P, 1], F32, name="baton")
         ident_f32 = const.tile([P, P], F32, name="ident_f32")
         ident_bf16 = const.tile([P, P], BF16, name="ident_bf16")
         b_rows = const.tile([P, P], BF16, name="b_rows")
@@ -96,12 +100,23 @@ def tile_slstmcell_kernel(tc, x_t, h_prev, c_prev, n_prev, W, R, b, out_0, out_1
             nc.sync.dma_start(out=raw[:], in_=rows.rearrange("(p t) w -> p t w", t=PACK))
             live["raw", u] = raw
 
-        def interleave(copy, u, w0, w1):
+        def new_grouped(u):
             if ("grouped", u) not in live:
                 grouped = grouped_pool.tile([P, STEP, PACK], BF16, name="grouped", align_bytes=64)
                 live["grouped", u] = grouped
+
+        def interleave(copy, u, w0, w1):
+            new_grouped(u)
             copy(out=live["grouped", u][:, w0:w1, :].rearrange("p (c i) t -> p c t i", i=4),
                  in_=live["raw", u][:, :, w0:w1].rearrange("p t (c i) -> p c t i", i=4))
+
+        def gpsimd_share(u):
+            w0 = VECTOR_COLUMNS[u]
+            w1 = w0 + GPSIMD_COLUMNS[u]
+            new_grouped(u)
+            nc.vector.memset(baton[:], 1.0)
+            nc.gpsimd.tensor_scalar(out=live["grouped", u][:, w0:w1, :], in0=live["raw", u][:, :, w0:w1].rearrange("p t w -> p w t"),
+                                    scalar1=baton[:], scalar2=0.0, op0=ALU.mult, op1=ALU.add)
 
         def quantise_unit(u):
             s, a = divmod(u, PASSES)
@@ -270,11 +285,14 @@ def tile_slstmcell_kernel(tc, x_t, h_prev, c_prev, n_prev, W, R, b, out_0, out_1
             if first % 4 == 0 and 0 <= first < N_ITEMS:
                 for e in range(first, first + 4):
                     gate_function(e)
-            if 0 <= u + 1 < N_UNITS and VECTOR_COLUMNS[u + 1] < STEP:
-                interleave(nc.scalar.copy, u + 1, VECTOR_COLUMNS[u + 1], STEP)
-            if j >= 0:
+            if 0 <= u + 1 < N_UNITS and VECTOR_COLUMNS[u + 1] + GPSIMD_COLUMNS[u + 1] < STEP:
+                interleave(nc.scalar.copy, u + 1, VECTOR_COLUMNS[u + 1] + GPSIMD_COLUMNS[u + 1], STEP)
+            if 0 <= j + GPSIMD_LEAD < N_UNITS and GPSIMD_COLUMNS[j + GPSIMD_LEAD] > 0:
+                gpsimd_share(j + GPSIMD_LEAD)
+            if j >= 0 and j % 2 == 0:
                 finish_item(j)
-                if gate_and_tile(j)[0] == G_Z and j % 4 == 3:
+                finish_item(j + 1)
+                if gate_and_tile(j)[0] == G_Z and j % 4 == 2:
                     cols = half_columns((j // 4) % 2)
                     nc.sync.dma_start(out=c_out[:, :, cols], in_=cell[:, :, cols])
             if j == LN_SLOT:
@@ -286,13 +304,15 @@ def tile_slstmcell_kernel(tc, x_t, h_prev, c_prev, n_prev, W, R, b, out_0, out_1
                     nc.scalar.activation(out=ratio[:, 2 * k:2 * k + 2, :], in_=ratio[:, 2 * k:2 * k + 2, :], func=AF.Exp,
                                          scale=-1.0)
             ahead = j + TURN_LEAD
-            if 0 <= ahead < N_ITEMS:
-                if gate_and_tile(ahead)[0] == G_Z:
-                    input_times_candidate(ahead)
+            turning = 0 <= ahead < N_ITEMS and j % 2 == 0
+            if turning and gate_and_tile(ahead)[0] == G_Z:
+                input_times_candidate(ahead)
+                input_times_candidate(ahead + 1)
             if j in SCALED_CELL_SLOTS:
                 scaled_cell(SCALED_CELL_SLOTS.index(j))
-            if 0 <= ahead < N_ITEMS:
+            if turning:
                 turn_item(ahead)
+                turn_item(ahead + 1)
             if 0 <= u - 1 < N_UNITS:
                 quantise_unit(u - 1)
                 if u - 1 < 2:

@@ -35,7 +35,7 @@ TURN_LEAD = 2
 LN_SLOT = 15
 EXP_SLOT = 18
 SCALED_CELL_SLOTS = (23, 27)
-SECOND_STATE_LOAD_AT = 10
+SECOND_STATE_LOAD_AT = 12
 
 RAW_BUFS = 8
 GROUPED_BUFS = 5
@@ -269,9 +269,10 @@ def tile_slstmcell_kernel(tc, x_t, h_prev, c_prev, n_prev, W, R, b, out_0, out_1
         load_unit(1)
         load_unit(2)
         load_unit(3)
-        load_state(0)
-        for u in range(4, RAW_BUFS):
+        for u in range(4, RAW_BUFS - 1):
             load_unit(u)
+        load_state(0)
+        load_unit(RAW_BUFS - 1)
         transpose_rows(0, 0)
         transpose_rows(0, 1)
         b_turn = turn_pool.tile([P, P], BF16, name="b_turn", tag="turn")
@@ -287,6 +288,8 @@ def tile_slstmcell_kernel(tc, x_t, h_prev, c_prev, n_prev, W, R, b, out_0, out_1
                     gate_function(e)
             if 0 <= u + 1 < N_UNITS and VECTOR_COLUMNS[u + 1] + GPSIMD_COLUMNS[u + 1] < STEP:
                 interleave(nc.scalar.copy, u + 1, VECTOR_COLUMNS[u + 1] + GPSIMD_COLUMNS[u + 1], STEP)
+            if j in (0, 4):
+                halve_n(j // 4)
             if 0 <= j + GPSIMD_LEAD < N_UNITS and GPSIMD_COLUMNS[j + GPSIMD_LEAD] > 0:
                 gpsimd_share(j + GPSIMD_LEAD)
             if j >= 0 and j % 2 == 0:
@@ -315,14 +318,12 @@ def tile_slstmcell_kernel(tc, x_t, h_prev, c_prev, n_prev, W, R, b, out_0, out_1
                 turn_item(ahead + 1)
             if 0 <= u - 1 < N_UNITS:
                 quantise_unit(u - 1)
-                if u - 1 < 2:
-                    quantise_rows(2 * (u - 1))
-                    quantise_rows(2 * (u - 1) + 1)
-                if u - 1 == 0:
+                if u - 1 in (1, 2):
+                    quantise_rows(2 * (u - 2))
+                    quantise_rows(2 * (u - 2) + 1)
+                if u - 1 == 1:
                     nc.vector.tensor_copy(out=bias[:], in_=b_turn[:, 0:32])
                     nc.vector.tensor_scalar_mul(out=bias_half[:], in0=b_turn[:, 16:32], scalar1=0.5)
-                if u - 1 in (3, 7):
-                    halve_n((u - 1) // 4)
                 following = u - 1 + RAW_BUFS
                 if following == SECOND_STATE_LOAD_AT:
                     load_state(1)
@@ -331,6 +332,9 @@ def tile_slstmcell_kernel(tc, x_t, h_prev, c_prev, n_prev, W, R, b, out_0, out_1
                 if following == N_UNITS - 1:
                     for half in range(2):
                         nc.sync.dma_start(out=n_out[:, :, half_columns(half)], in_=norm[:, :, half_columns(half)])
-                multiply_pass(u - 1)
+                if u - 1 == 1:
+                    multiply_pass(0)
+                if u - 1 > 0:
+                    multiply_pass(u - 1)
             if 0 <= u < N_UNITS and VECTOR_COLUMNS[u] > 0:
                 interleave(nc.vector.tensor_copy, u, 0, VECTOR_COLUMNS[u])

@@ -25,7 +25,7 @@ N_ITEMS = 4 * H // P
 G_F, G_I, G_Z, G_O = 0, 1, 2, 3
 COLUMN_BLOCK = (2, 1, 0, 3)
 
-VECTOR_COLUMNS = (512,) * 6 + (144,) * 2 + (32, 64) * 4 + (208, 240) * 4 + (384, 512) * 2 + (64, 64) * 2
+VECTOR_COLUMNS = (512,) * 4 + (256,) * 2 + (144,) * 2 + (32, 64) * 4 + (208, 240) * 4 + (384, 512) * 2 + (64, 64) * 2
 
 GPSIMD_COLUMNS = (0,) * 8 + (352, 0) * 4 + (128, 0) * 8
 GPSIMD_LEAD = 8
@@ -263,10 +263,10 @@ def tile_slstmcell_kernel(tc, x_t, h_prev, c_prev, n_prev, W, R, b, out_0, out_1
         nc.gpsimd.memset(b_rows[:], 0.0)
         make_identity(nc, ident_f32[:])
         make_identity(nc, ident_bf16[:])
+        load_unit(1)
         nc.sync.dma_start(out=b_rows[0:4 * H // P, :], in_=b.rearrange("(t c) -> t c", c=P))
         load_rows(1, 0)
         load_rows(1, 1)
-        load_unit(1)
         load_unit(2)
         load_unit(3)
         for u in range(4, RAW_BUFS - 1):
@@ -318,9 +318,9 @@ def tile_slstmcell_kernel(tc, x_t, h_prev, c_prev, n_prev, W, R, b, out_0, out_1
                 turn_item(ahead + 1)
             if 0 <= u - 1 < N_UNITS:
                 quantise_unit(u - 1)
-                if u - 1 in (1, 2):
-                    quantise_rows(2 * (u - 2))
-                    quantise_rows(2 * (u - 2) + 1)
+                if u - 1 in (1, 3):
+                    quantise_rows(u - 2)
+                    quantise_rows(u - 1)
                 if u - 1 == 1:
                     nc.vector.tensor_copy(out=bias[:], in_=b_turn[:, 0:32])
                     nc.vector.tensor_scalar_mul(out=bias_half[:], in0=b_turn[:, 16:32], scalar1=0.5)
@@ -332,9 +332,9 @@ def tile_slstmcell_kernel(tc, x_t, h_prev, c_prev, n_prev, W, R, b, out_0, out_1
                 if following == N_UNITS - 1:
                     for half in range(2):
                         nc.sync.dma_start(out=n_out[:, :, half_columns(half)], in_=norm[:, :, half_columns(half)])
-                if u - 1 == 1:
-                    multiply_pass(0)
-                if u - 1 > 0:
+                if u - 1 in (1, 3):
+                    multiply_pass(u - 2)
+                if u - 1 not in (0, 2):
                     multiply_pass(u - 1)
             if 0 <= u < N_UNITS and VECTOR_COLUMNS[u] > 0:
                 interleave(nc.vector.tensor_copy, u, 0, VECTOR_COLUMNS[u])

@@ -25,7 +25,7 @@ N_ITEMS = 4 * H // P
 G_F, G_I, G_Z, G_O = 0, 1, 2, 3
 COLUMN_BLOCK = (2, 1, 0, 3)
 
-VECTOR_COLUMNS = (512,) * 4 + (256,) * 2 + (144,) * 2 + (32, 64) * 4 + (208, 240) * 4 + (384, 512) * 2 + (64, 64) * 2
+VECTOR_COLUMNS = (512,) * 4 + (256,) * 2 + (144,) * 2 + (32, 64) * 4 + (208, 240) * 4 + (384, 512, 256, 288) + (64, 64) * 2
 
 GPSIMD_COLUMNS = (0,) * 8 + (352, 0) * 4 + (128, 0) * 8
 GPSIMD_LEAD = 8
@@ -33,7 +33,7 @@ GPSIMD_LEAD = 8
 LEAD = 7
 TURN_LEAD = 2
 LN_SLOT = 15
-EXP_SLOT = 18
+EXP_SLOTS = (18, 24)
 SCALED_CELL_SLOTS = (23, 27)
 SECOND_STATE_LOAD_AT = 12
 
@@ -302,10 +302,9 @@ def tile_slstmcell_kernel(tc, x_t, h_prev, c_prev, n_prev, W, R, b, out_0, out_1
                 for k in range(2):
                     nc.scalar.activation(out=ratio[:, 2 * k:2 * k + 2, :], in_=norm[:, 2 * k:2 * k + 2, :], func=AF.Ln,
                                          bias=1e-6, scale=1.0)
-            if j == EXP_SLOT:
-                for k in range(2):
-                    nc.scalar.activation(out=ratio[:, 2 * k:2 * k + 2, :], in_=ratio[:, 2 * k:2 * k + 2, :], func=AF.Exp,
-                                         scale=-1.0)
+            if j in EXP_SLOTS:
+                cols = half_columns(EXP_SLOTS.index(j))
+                nc.scalar.activation(out=ratio[:, :, cols], in_=ratio[:, :, cols], func=AF.Exp, scale=-1.0)
             ahead = j + TURN_LEAD
             turning = 0 <= ahead < N_ITEMS and j % 2 == 0
             if turning and gate_and_tile(ahead)[0] == G_Z:

@@ -315,6 +315,9 @@ def tile_slstmcell_kernel(tc, x_t, h_prev, c_prev, n_prev, W, R, b, out_0, out_1
             if turning:
                 turn_item(ahead)
                 turn_item(ahead + 1)
+            copy_first = j > 0 and j % 2 == 1
+            if copy_first and u < N_UNITS and VECTOR_COLUMNS[u] > 0:
+                interleave(nc.vector.tensor_copy, u, 0, VECTOR_COLUMNS[u])
             if 0 <= u - 1 < N_UNITS:
                 quantise_unit(u - 1)
                 if u - 1 in (1, 3):
@@ -335,5 +338,5 @@ def tile_slstmcell_kernel(tc, x_t, h_prev, c_prev, n_prev, W, R, b, out_0, out_1
                     multiply_pass(u - 2)
                 if u - 1 not in (0, 2):
                     multiply_pass(u - 1)
-            if 0 <= u < N_UNITS and VECTOR_COLUMNS[u] > 0:
+            if not copy_first and 0 <= u < N_UNITS and VECTOR_COLUMNS[u] > 0:
                 interleave(nc.vector.tensor_copy, u, 0, VECTOR_COLUMNS[u])

@@ -25,7 +25,7 @@ N_ITEMS = 4 * H // P
 G_F, G_I, G_Z, G_O = 0, 1, 2, 3
 COLUMN_BLOCK = (2, 1, 0, 3)
 
-VECTOR_COLUMNS = (512,) * 4 + (256,) * 2 + (144,) * 2 + (32, 64) * 4 + (208, 240) * 4 + (384, 512, 256, 288) + (64, 64) * 2
+VECTOR_COLUMNS = (512,) * 4 + (256,) * 2 + (144,) * 2 + (64, 32) * 4 + (272, 240) * 4 + (384, 512, 256, 288) + (64, 64) * 2
 
 GPSIMD_COLUMNS = (0,) * 8 + (352, 0) * 4 + (128, 0) * 8
 GPSIMD_LEAD = 8
@@ -315,7 +315,7 @@ def tile_slstmcell_kernel(tc, x_t, h_prev, c_prev, n_prev, W, R, b, out_0, out_1
             if turning:
                 turn_item(ahead)
                 turn_item(ahead + 1)
-            copy_first = j > 0 and j % 2 == 1
+            copy_first = (j > 0 and j % 2 == 1) or -4 <= j < 0
             if copy_first and u < N_UNITS and VECTOR_COLUMNS[u] > 0:
                 interleave(nc.vector.tensor_copy, u, 0, VECTOR_COLUMNS[u])
             if 0 <= u - 1 < N_UNITS:

@@ -24,18 +24,19 @@ N_UNITS = 8 * PASSES
 N_ITEMS = 4 * H // P
 G_F, G_I, G_Z, G_O = 0, 1, 2, 3
 COLUMN_BLOCK = (2, 1, 0, 3)
+STEP_ORDER = ((G_F, 0), (G_I, 0), (G_F, 1), (G_I, 1), (G_Z, 0), (G_Z, 1), (G_O, 0), (G_O, 1))
 
-VECTOR_COLUMNS = (512,) * 4 + (256,) * 2 + (144,) * 2 + (64, 32) * 4 + (272, 240) * 4 + (384, 512, 256, 288) + (64, 64) * 2
+VECTOR_COLUMNS = (512,) * 4 + (256,) * 2 + (144,) * 2 + (64, 32) * 2 + (272, 240, 272, 128) + (64, 32) * 2 + (272, 240) * 2 + (512, 384, 288, 256) + (64, 64) * 2
 
-GPSIMD_COLUMNS = (0,) * 8 + (352, 0) * 4 + (128, 0) * 8
-GPSIMD_LEAD = 8
+GPSIMD_COLUMNS = (0,) * 6 + ((0, 352) * 2 + (0, 128) * 2) * 2 + (0, 128) * 5
+GPSIMD_LEAD = 7
 
 LEAD = 7
 TURN_LEAD = 2
 LN_SLOT = 15
 EXP_SLOTS = (18, 24)
 SCALED_CELL_SLOTS = (23, 27)
-SECOND_STATE_LOAD_AT = 12
+SECOND_STATE_LOAD_AT = 15
 
 RAW_BUFS = 8
 GROUPED_BUFS = 5
@@ -85,15 +86,16 @@ def tile_slstmcell_kernel(tc, x_t, h_prev, c_prev, n_prev, W, R, b, out_0, out_1
         live = {}
 
         def gate_and_tile(e):
-            s = e // 4
-            return s // 2, (s % 2) * 4 + e % 4
+            gate, half = STEP_ORDER[e // 4]
+            return gate, half * 4 + e % 4
 
         def half_columns(half):
             return slice(half * STEP, (half + 1) * STEP)
 
         def load_unit(u):
             s, a = divmod(u, PASSES)
-            col0 = COLUMN_BLOCK[s // 2] * H + (s % 2) * STEP
+            gate, half = STEP_ORDER[s]
+            col0 = COLUMN_BLOCK[gate] * H + half * STEP
             row0 = (a % 2) * K_PASS
             rows = (W if a < 2 else R)[row0:row0 + K_PASS, col0:col0 + STEP]
             raw = raw_pool.tile([P, PACK, STEP], BF16, name="raw")
@@ -288,8 +290,8 @@ def tile_slstmcell_kernel(tc, x_t, h_prev, c_prev, n_prev, W, R, b, out_0, out_1
                     gate_function(e)
             if 0 <= u + 1 < N_UNITS and VECTOR_COLUMNS[u + 1] + GPSIMD_COLUMNS[u + 1] < STEP:
                 interleave(nc.scalar.copy, u + 1, VECTOR_COLUMNS[u + 1] + GPSIMD_COLUMNS[u + 1], STEP)
-            if j in (0, 4):
-                halve_n(j // 4)
+            if j in (0, 8):
+                halve_n(j // 8)
             if 0 <= j + GPSIMD_LEAD < N_UNITS and GPSIMD_COLUMNS[j + GPSIMD_LEAD] > 0:
                 gpsimd_share(j + GPSIMD_LEAD)
             if j >= 0 and j % 2 == 0:

@@ -26,9 +26,9 @@ G_F, G_I, G_Z, G_O = 0, 1, 2, 3
 COLUMN_BLOCK = (2, 1, 0, 3)
 STEP_ORDER = ((G_F, 0), (G_I, 0), (G_F, 1), (G_I, 1), (G_Z, 0), (G_Z, 1), (G_O, 0), (G_O, 1))
 
-VECTOR_COLUMNS = (512,) * 4 + (256,) * 2 + (144,) * 2 + (64, 32) * 2 + (272, 240, 272, 128) + (64, 32) * 2 + (272, 240) * 2 + (512, 384, 288, 256) + (64, 64) * 2
+VECTOR_COLUMNS = (512,) * 4 + (256,) * 2 + (144,) * 2 + (64, 32) * 2 + (224, 192, 224, 128) + (64, 32) * 2 + (224, 192) * 2 + (464, 336, 240, 208) + (64, 64) * 2
 
-GPSIMD_COLUMNS = (0,) * 6 + ((0, 352) * 2 + (0, 128) * 2) * 2 + (0, 128) * 5
+GPSIMD_COLUMNS = (0,) * 6 + (0, 352, 0, 400) + (0, 176) * 2 + (0, 384, 0, 400) + (0, 176) * 2 + (0, 176) * 5
 GPSIMD_LEAD = 7
 
 LEAD = 7
@@ -247,15 +247,23 @@ def tile_slstmcell_kernel(tc, x_t, h_prev, c_prev, n_prev, W, R, b, out_0, out_1
                 if not second:
                     h_tile = h_pool.tile([P, ROWS, 2 * P], F32, name="h_tile")
                     live["h_tile"] = h_tile
-                stt(out=live["h_tile"][:, :, second * P:(second + 1) * P], in0=turn[:], scalar=1.0,
-                    in1=ratio[:, :, cols], op0=ALU.add, op1=ALU.mult)
-                if second:
-                    nc.sync.dma_start(out=h_out[:, :, pair * 2 * P:(pair + 1) * 2 * P], in_=live.pop("h_tile")[:])
+                own = slice(second * P, (second + 1) * P)
+                if e < N_ITEMS - 2:
+                    stt(out=live["h_tile"][:, :, own], in0=turn[:], scalar=1.0, in1=ratio[:, :, cols], op0=ALU.add, op1=ALU.mult)
+                    if second:
+                        nc.sync.dma_start(out=h_out[:, :, pair * 2 * P:(pair + 1) * 2 * P], in_=live.pop("h_tile")[:])
+                else:
+                    pieces = ((0, ROWS),) if e < N_ITEMS - 1 else ((0, ROWS // 2), (ROWS // 2, ROWS))
+                    for t0, t1 in pieces:
+                        stt(out=live["h_tile"][:, t0:t1, own], in0=turn[:, t0:t1, :], scalar=1.0, in1=ratio[:, t0:t1, cols],
+                            op0=ALU.add, op1=ALU.mult)
+                        nc.sync.dma_start(out=h_out[:, t0:t1, cols], in_=live["h_tile"][:, t0:t1, own])
 
         def scaled_cell(half):
-            cols = half_columns(half)
-            stt(out=ratio[:, :, cols], in0=cell[:, :, cols], scalar=0.5, in1=ratio[:, :, cols],
-                op0=ALU.mult, op1=ALU.mult)
+            for quarter in (2 * half, 2 * half + 1):
+                cols = slice(quarter * 2 * P, (quarter + 1) * 2 * P)
+                stt(out=ratio[:, :, cols], in0=cell[:, :, cols], scalar=0.5, in1=ratio[:, :, cols],
+                    op0=ALU.mult, op1=ALU.mult)
 
         load_rows(0, 0)
         load_rows(0, 1)
@@ -292,7 +300,7 @@ def tile_slstmcell_kernel(tc, x_t, h_prev, c_prev, n_prev, W, R, b, out_0, out_1
                 interleave(nc.scalar.copy, u + 1, VECTOR_COLUMNS[u + 1] + GPSIMD_COLUMNS[u + 1], STEP)
             if j in (0, 8):
                 halve_n(j // 8)
-            if 0 <= j + GPSIMD_LEAD < N_UNITS and GPSIMD_COLUMNS[j + GPSIMD_LEAD] > 0:
+            if j in (0, 8):
                 gpsimd_share(j + GPSIMD_LEAD)
             if j >= 0 and j % 2 == 0:
                 finish_item(j)
@@ -320,6 +328,9 @@ def tile_slstmcell_kernel(tc, x_t, h_prev, c_prev, n_prev, W, R, b, out_0, out_1
             copy_first = (j > 0 and j % 2 == 1) or -4 <= j < 0
             if copy_first and u < N_UNITS and VECTOR_COLUMNS[u] > 0:
                 interleave(nc.vector.tensor_copy, u, 0, VECTOR_COLUMNS[u])
+            next_share = j + 1 + GPSIMD_LEAD
+            if j + 1 not in (0, 8) and 0 <= next_share < N_UNITS and GPSIMD_COLUMNS[next_share] > 0:
+                gpsimd_share(next_share)
             if 0 <= u - 1 < N_UNITS:
                 quantise_unit(u - 1)
                 if u - 1 in (1, 3):

@@ -33,6 +33,7 @@ GPSIMD_LEAD = 7
 
 LEAD = 7
 TURN_LEAD = 2
+LN_2 = 0.6931471805599453
 LN_SLOT = 15
 EXP_SLOTS = (18, 24)
 SCALED_CELL_SLOTS = (23, 27)
@@ -120,6 +121,12 @@ def tile_slstmcell_kernel(tc, x_t, h_prev, c_prev, n_prev, W, R, b, out_0, out_1
             nc.gpsimd.tensor_scalar(out=live["grouped", u][:, w0:w1, :], in0=live["raw", u][:, :, w0:w1].rearrange("p t w -> p w t"),
                                     scalar1=baton[:], scalar2=0.0, op0=ALU.mult, op1=ALU.add)
 
+        def gpsimd_share_behind_copy(u):
+            w0 = VECTOR_COLUMNS[u] - 4
+            w1 = VECTOR_COLUMNS[u] + GPSIMD_COLUMNS[u]
+            nc.gpsimd.tensor_scalar(out=live["grouped", u][:, w0:w1, :], in0=live["raw", u][:, :, w0:w1].rearrange("p t w -> p w t"),
+                                    scalar1=1.0, scalar2=0.0, op0=ALU.mult, op1=ALU.add)
+
         def quantise_unit(u):
             s, a = divmod(u, PASSES)
             if a == 0:
@@ -127,12 +134,13 @@ def tile_slstmcell_kernel(tc, x_t, h_prev, c_prev, n_prev, W, R, b, out_0, out_1
                 scales = code_pool.tile([P, PASSES, STEP], U8, name="scales", align_bytes=64)
                 live["codes", s] = (codes, scales)
             codes, scales = live["codes", s]
+            live["last_grouped"] = live.pop(("grouped", u))
             nc.vector.quantize_mx(
                 out=codes[:, a, :].bitcast(E5M2X4),
                 scales=scales[:, a, :],
-                in_=live.pop(("grouped", u))[:].rearrange("p w t -> p (w t)"),
+                in_=live["last_grouped"][:].rearrange("p w t -> p (w t)"),
             )
-            live.pop(("raw", u))
+            live["last_raw"] = live.pop(("raw", u))
 
         def load_rows(i, pair):
             if pair == 0:
@@ -260,10 +268,15 @@ def tile_slstmcell_kernel(tc, x_t, h_prev, c_prev, n_prev, W, R, b, out_0, out_1
                         nc.sync.dma_start(out=h_out[:, t0:t1, cols], in_=live["h_tile"][:, t0:t1, own])
 
         def scaled_cell(half):
-            for quarter in (2 * half, 2 * half + 1):
-                cols = slice(quarter * 2 * P, (quarter + 1) * 2 * P)
-                stt(out=ratio[:, :, cols], in0=cell[:, :, cols], scalar=0.5, in1=ratio[:, :, cols],
-                    op0=ALU.mult, op1=ALU.mult)
+            for c0, c1 in (((0, 2), (2, 4)), ((4, 6), (6, 7)))[half]:
+                cols = slice(c0 * P, c1 * P)
+                nc.vector.tensor_mul(out=ratio[:, :, cols], in0=cell[:, :, cols], in1=ratio[:, :, cols])
+
+        def scaled_cell_on_gpsimd():
+            nc.gpsimd.tensor_scalar(out=live["last_grouped"][:, 0:4, :], in0=live["last_raw"][:, :, 0:4].rearrange("p t w -> p w t"),
+                                    scalar1=1.0, scalar2=0.0, op0=ALU.mult, op1=ALU.add)
+            cols = slice(H - P, H)
+            nc.gpsimd.tensor_tensor(out=ratio[:, :, cols], in0=cell[:, :, cols], in1=ratio[:, :, cols], op=ALU.mult)
 
         load_rows(0, 0)
         load_rows(0, 1)
@@ -314,7 +327,7 @@ def tile_slstmcell_kernel(tc, x_t, h_prev, c_prev, n_prev, W, R, b, out_0, out_1
                                          bias=1e-6, scale=1.0)
             if j in EXP_SLOTS:
                 cols = half_columns(EXP_SLOTS.index(j))
-                nc.scalar.activation(out=ratio[:, :, cols], in_=ratio[:, :, cols], func=AF.Exp, scale=-1.0)
+                nc.scalar.activation(out=ratio[:, :, cols], in_=ratio[:, :, cols], func=AF.Exp, bias=-LN_2, scale=-1.0)
             ahead = j + TURN_LEAD
             turning = 0 <= ahead < N_ITEMS and j % 2 == 0
             if turning and gate_and_tile(ahead)[0] == G_Z:
@@ -330,9 +343,13 @@ def tile_slstmcell_kernel(tc, x_t, h_prev, c_prev, n_prev, W, R, b, out_0, out_1
                 interleave(nc.vector.tensor_copy, u, 0, VECTOR_COLUMNS[u])
             next_share = j + 1 + GPSIMD_LEAD
             if j + 1 not in (0, 8) and 0 <= next_share < N_UNITS and GPSIMD_COLUMNS[next_share] > 0:
-                gpsimd_share(next_share)
+                interleave(nc.vector.tensor_copy, next_share, 0, VECTOR_COLUMNS[next_share])
+                gpsimd_share_behind_copy(next_share)
+                live["copied", next_share] = True
             if 0 <= u - 1 < N_UNITS:
                 quantise_unit(u - 1)
+                if u - 1 == N_UNITS - 1:
+                    scaled_cell_on_gpsimd()
                 if u - 1 in (1, 3):
                     quantise_rows(u - 2)
                     quantise_rows(u - 1)
@@ -351,5 +368,5 @@ def tile_slstmcell_kernel(tc, x_t, h_prev, c_prev, n_prev, W, R, b, out_0, out_1
                     multiply_pass(u - 2)
                 if u - 1 not in (0, 2):
                     multiply_pass(u - 1)
-            if not copy_first and 0 <= u < N_UNITS and VECTOR_COLUMNS[u] > 0:
+            if not copy_first and 0 <= u < N_UNITS and VECTOR_COLUMNS[u] > 0 and ("copied", u) not in live:
                 interleave(nc.vector.tensor_copy, u, 0, VECTOR_COLUMNS[u])

@@ -26,9 +26,9 @@ G_F, G_I, G_Z, G_O = 0, 1, 2, 3
 COLUMN_BLOCK = (2, 1, 0, 3)
 STEP_ORDER = ((G_F, 0), (G_I, 0), (G_F, 1), (G_I, 1), (G_Z, 0), (G_Z, 1), (G_O, 0), (G_O, 1))
 
-VECTOR_COLUMNS = (512,) * 4 + (256,) * 2 + (144,) * 2 + (64, 32) * 2 + (224, 192, 224, 128) + (64, 32) * 2 + (224, 192) * 2 + (464, 336, 240, 208) + (64, 64) * 2
+VECTOR_COLUMNS = (512,) * 4 + (256,) * 2 + (144,) * 2 + (96, 32) * 2 + (288, 232, 288, 128) + (96, 32) * 2 + (288, 232) * 2 + (512, 312, 304, 248) + (96, 40) * 2
 
-GPSIMD_COLUMNS = (0,) * 6 + (0, 352, 0, 400) + (0, 176) * 2 + (0, 384, 0, 400) + (0, 176) * 2 + (0, 176) * 5
+GPSIMD_COLUMNS = (0,) * 6 + (0, 352, 0, 408) + (0, 200) * 2 + (0, 384, 0, 408) + (0, 200) * 2 + (0, 200) * 5
 GPSIMD_LEAD = 7
 
 LEAD = 7

@@ -26,7 +26,7 @@ G_F, G_I, G_Z, G_O = 0, 1, 2, 3
 COLUMN_BLOCK = (2, 1, 0, 3)
 STEP_ORDER = ((G_F, 0), (G_I, 0), (G_F, 1), (G_I, 1), (G_Z, 0), (G_Z, 1), (G_O, 0), (G_O, 1))
 
-VECTOR_COLUMNS = (512,) * 4 + (256,) * 2 + (144,) * 2 + (96, 32) * 2 + (288, 232, 288, 128) + (96, 32) * 2 + (288, 232) * 2 + (512, 312, 304, 248) + (96, 40) * 2
+VECTOR_COLUMNS = (512,) * 4 + (256,) * 2 + (144,) * 2 + (32, 32, 160, 32) + (224, 232, 352, 128) + (32, 32, 160, 32) + (224, 232, 352, 232) + (512, 312, 304, 248) + (32, 40, 160, 40)
 
 GPSIMD_COLUMNS = (0,) * 6 + (0, 352, 0, 408) + (0, 200) * 2 + (0, 384, 0, 408) + (0, 200) * 2 + (0, 200) * 5
 GPSIMD_LEAD = 7

from contextlib import ExitStack

import concourse.mybir as mybir
from concourse.masks import make_identity

F32 = mybir.dt.float32
BF16 = mybir.dt.bfloat16
U32 = mybir.dt.uint32
U8 = mybir.dt.uint8
E5M2X4 = mybir.dt.float8_e5m2_x4
AF = mybir.ActivationFunctionType
ALU = mybir.AluOpType

B, D, H = 512, 1024, 1024
FLOPS = 2 * B * (D + H) * 4 * H

P = 128
PACK = 4
K_PASS = P * PACK
ROWS = B // P
STEP = 512
PASSES = (D + H) // K_PASS
N_UNITS = 8 * PASSES
N_ITEMS = 4 * H // P
G_F, G_I, G_Z, G_O = 0, 1, 2, 3
COLUMN_BLOCK = (2, 1, 0, 3)
STEP_ORDER = ((G_F, 0), (G_I, 0), (G_F, 1), (G_I, 1), (G_Z, 0), (G_Z, 1), (G_O, 0), (G_O, 1))

VECTOR_COLUMNS = (512,) * 4 + (256,) * 2 + (144,) * 2 + (32, 32, 160, 32) + (224, 232, 352, 128) + (32, 32, 160, 32) + (224, 232, 352, 232) + (512, 312, 304, 248) + (32, 40, 160, 40)

GPSIMD_COLUMNS = (0,) * 6 + (0, 352, 0, 408) + (0, 200) * 2 + (0, 384, 0, 408) + (0, 200) * 2 + (0, 200) * 5
GPSIMD_LEAD = 7

LEAD = 7
TURN_LEAD = 2
LN_2 = 0.6931471805599453
LN_SLOT = 15
EXP_SLOTS = (18, 24)
SCALED_CELL_SLOTS = (23, 27)
SECOND_STATE_LOAD_AT = 15

RAW_BUFS = 8
GROUPED_BUFS = 5
CODE_BUFS = 3
GATE_BUFS = 6
PRODUCT_BUFS = 3


def tile_slstmcell_kernel(tc, x_t, h_prev, c_prev, n_prev, W, R, b, out_0, out_1, out_2):
    nc = tc.nc
    stt = nc.vector.scalar_tensor_tensor
    with ExitStack() as ctx:
        const = ctx.enter_context(tc.tile_pool(name="const", bufs=1))
        keep = ctx.enter_context(tc.tile_pool(name="keep", bufs=1))
        raw_pool = ctx.enter_context(tc.tile_pool(name="raw_pool", bufs=RAW_BUFS))
        rows_pool = ctx.enter_context(tc.tile_pool(name="rows_pool", bufs=2))
        rows_grouped_pool = ctx.enter_context(tc.tile_pool(name="rows_grouped_pool", bufs=2))
        grouped_pool = ctx.enter_context(tc.tile_pool(name="grouped_pool", bufs=GROUPED_BUFS))
        code_pool = ctx.enter_context(tc.tile_pool(name="code_pool", bufs=CODE_BUFS))
        gate_pool = ctx.enter_context(tc.tile_pool(name="gate_pool", bufs=GATE_BUFS))
        product_pool = ctx.enter_context(tc.tile_pool(name="product_pool", bufs=PRODUCT_BUFS))
        h_pool = ctx.enter_context(tc.tile_pool(name="h_pool", bufs=2))
        sum_pool = ctx.enter_context(tc.psum_pool(name="sum_pool", bufs=4))
        turn_pool = ctx.enter_context(tc.psum_pool(name="turn_pool", bufs=4))
        ctx.enter_context(tc.manual_schedule())

        table_warmer = const.tile([P, 1], F32, name="table_warmer")
        baton = const.tile([P, 1], F32, name="baton")
        ident_f32 = const.tile([P, P], F32, name="ident_f32")
        ident_bf16 = const.tile([P, P], BF16, name="ident_bf16")
        b_rows = const.tile([P, P], BF16, name="b_rows")
        bias = const.tile([P, 4 * H // P], F32, name="bias")
        bias_half = const.tile([P, 2 * H // P], F32, name="bias_half")
        c_sb = keep.tile([P, ROWS, H], BF16, name="c_sb")
        n_half = keep.tile([P, ROWS, H], BF16, name="n_half")
        cell = keep.tile([P, ROWS, H], F32, name="cell")
        norm = keep.tile([P, ROWS, H], F32, name="norm")
        ratio = keep.tile([P, ROWS, H], F32, name="ratio")
        exp_i = keep.tile([P, H // P, B], F32, name="exp_i")
        x_codes = keep.tile([P, PASSES, B], U32, name="x_codes", align_bytes=64)
        x_scales = keep.tile([P, PASSES, B], U8, name="x_scales", align_bytes=64)

        c_view = c_prev.rearrange("(p t) c -> p t c", t=ROWS)
        n_view = n_prev.rearrange("(p t) c -> p t c", t=ROWS)
        h_out, c_out, n_out = [o.rearrange("(p t) c -> p t c", t=ROWS) for o in (out_0, out_1, out_2)]

        live = {}

        def gate_and_tile(e):
            gate, half = STEP_ORDER[e // 4]
            return gate, half * 4 + e % 4

        def half_columns(half):
            return slice(half * STEP, (half + 1) * STEP)

        def load_unit(u):
            s, a = divmod(u, PASSES)
            gate, half = STEP_ORDER[s]
            col0 = COLUMN_BLOCK[gate] * H + half * STEP
            row0 = (a % 2) * K_PASS
            rows = (W if a < 2 else R)[row0:row0 + K_PASS, col0:col0 + STEP]
            raw = raw_pool.tile([P, PACK, STEP], BF16, name="raw")
            nc.sync.dma_start(out=raw[:], in_=rows.rearrange("(p t) w -> p t w", t=PACK))
            live["raw", u] = raw

        def new_grouped(u):
            if ("grouped", u) not in live:
                grouped = grouped_pool.tile([P, STEP, PACK], BF16, name="grouped", align_bytes=64)
                live["grouped", u] = grouped

        def interleave(copy, u, w0, w1):
            new_grouped(u)
            copy(out=live["grouped", u][:, w0:w1, :].rearrange("p (c i) t -> p c t i", i=4),
                 in_=live["raw", u][:, :, w0:w1].rearrange("p t (c i) -> p c t i", i=4))

        def gpsimd_share(u):
            w0 = VECTOR_COLUMNS[u]
            w1 = w0 + GPSIMD_COLUMNS[u]
            new_grouped(u)
            nc.vector.memset(baton[:], 1.0)
            nc.gpsimd.tensor_scalar(out=live["grouped", u][:, w0:w1, :], in0=live["raw", u][:, :, w0:w1].rearrange("p t w -> p w t"),
                                    scalar1=baton[:], scalar2=0.0, op0=ALU.mult, op1=ALU.add)

        def gpsimd_share_behind_copy(u):
            w0 = VECTOR_COLUMNS[u] - 4
            w1 = VECTOR_COLUMNS[u] + GPSIMD_COLUMNS[u]
            nc.gpsimd.tensor_scalar(out=live["grouped", u][:, w0:w1, :], in0=live["raw", u][:, :, w0:w1].rearrange("p t w -> p w t"),
                                    scalar1=1.0, scalar2=0.0, op0=ALU.mult, op1=ALU.add)

        def quantise_unit(u):
            s, a = divmod(u, PASSES)
            if a == 0:
                codes = code_pool.tile([P, PASSES, STEP], U32, name="codes", align_bytes=64)
                scales = code_pool.tile([P, PASSES, STEP], U8, name="scales", align_bytes=64)
                live["codes", s] = (codes, scales)
            codes, scales = live["codes", s]
            live["last_grouped"] = live.pop(("grouped", u))
            nc.vector.quantize_mx(
                out=codes[:, a, :].bitcast(E5M2X4),
                scales=scales[:, a, :],
                in_=live["last_grouped"][:].rearrange("p w t -> p (w t)"),
            )
            live["last_raw"] = live.pop(("raw", u))

        def load_rows(i, pair):
            if pair == 0:
                rows_in = rows_pool.tile([P, ROWS, D], BF16, name="rows_in")
                live["rows_in", i] = rows_in
            view = (x_t, h_prev)[i].rearrange("(p t) k -> p t k", t=ROWS)
            nc.sync.dma_start(out=live["rows_in", i][:, 2 * pair:2 * pair + 2, :], in_=view[:, 2 * pair:2 * pair + 2, :])

        def transpose_rows(i, pair):
            words = live["rows_in", i][:].bitcast(F32)
            turned = []
            for g in range(2):
                turn = turn_pool.tile([P, 2, 2 * P], F32, name="turn")
                for u in range(2):
                    for r in range(2):
                        nc.tensor.transpose(
                            turn[:, u, r * P:(r + 1) * P],
                            words[:, 2 * pair + r, 256 * g + u:256 * (g + 1):2],
                            ident_f32[:],
                        )
                turned.append(turn)
            for g in range(2):
                a = 2 * i + g
                if pair == 0:
                    rows_grouped = rows_grouped_pool.tile([P, B, PACK], BF16, name="rows_grouped", align_bytes=64)
                    live["rows_grouped", a] = rows_grouped
                as_words = live["rows_grouped", a][:].rearrange("p r t -> p (r t)").bitcast(F32)
                nc.scalar.copy(
                    out=as_words.rearrange("p (r u) -> p r u", u=2)[:, pair * 2 * P:(pair + 1) * 2 * P, :],
                    in_=turned[g][:].rearrange("p u r -> p r u"),
                )

        def quantise_rows(a):
            nc.vector.quantize_mx(
                out=x_codes[:, a, :].bitcast(E5M2X4),
                scales=x_scales[:, a, :],
                in_=live.pop(("rows_grouped", a))[:].rearrange("p r t -> p (r t)"),
            )

        def load_state(half):
            cols = half_columns(half)
            nc.sync.dma_start(out=c_sb[:, :, cols], in_=c_view[:, :, cols])
            nc.sync.dma_start(out=n_half[:, :, cols], in_=n_view[:, :, cols])

        def halve_n(half):
            cols = half_columns(half)
            nc.vector.tensor_scalar_mul(out=n_half[:, :, cols], in0=n_half[:, :, cols], scalar1=0.5)

        def multiply_pass(u):
            s, a = divmod(u, PASSES)
            codes, scales = live["codes", s]
            for k in range(4):
                e = 4 * s + k
                if a == 0:
                    sums = sum_pool.tile([P, B], F32, name="sums")
                    live["sums", e] = sums
                channels = slice(k * P, (k + 1) * P)
                nc.tensor.matmul_mx(
                    out=live["sums", e][:],
                    lhsT=codes[:, a, channels].bitcast(E5M2X4),
                    lhsT_scale=scales[:, a, channels],
                    rhs=x_codes[:, a, :].bitcast(E5M2X4),
                    rhs_scale=x_scales[:, a, :],
                    start=(a == 0),
                    stop=(a == PASSES - 1),
                )

        def gate_function(e):
            gate, c = gate_and_tile(e)
            sums = live.pop(("sums", e))
            if gate == G_I:
                nc.scalar.activation(out=exp_i[:, c, :], in_=sums[:], func=AF.Exp,
                                     bias=bias[:, 8 + c:9 + c], scale=1.0)
                return
            value = gate_pool.tile([P, B], F32, name="value")
            if gate == G_Z:
                nc.scalar.activation(out=value[:], in_=sums[:], func=AF.Tanh, bias=bias[:, c:c + 1], scale=1.0)
            else:
                col = c if gate == G_F else 8 + c
                nc.scalar.activation(out=value[:], in_=sums[:], func=AF.Tanh, bias=bias_half[:, col:col + 1],
                                     scale=0.5)
            live["value", e] = value

        def input_times_candidate(e):
            c = gate_and_tile(e)[1]
            product = product_pool.tile([P, B], F32, name="product")
            stt(out=product[:], in0=exp_i[:, c, :], scalar=50.0, in1=live.pop(("value", e))[:],
                op0=ALU.min, op1=ALU.mult)
            live["value", e] = product

        def turn_item(e):
            gate, c = gate_and_tile(e)
            src = exp_i[:, c, :] if gate == G_I else live.pop(("value", e))[:]
            turn = turn_pool.tile([P, ROWS, P], F32, name="turn")
            for t in range(ROWS):
                nc.tensor.transpose(turn[:, t, :], src[:, t * P:(t + 1) * P], ident_f32[:])
            live["turn", e] = turn

        def finish_item(e):
            gate, c = gate_and_tile(e)
            cols = slice(c * P, (c + 1) * P)
            turn = live.pop(("turn", e))
            if gate == G_F:
                stt(out=cell[:, :, cols], in0=turn[:], scalar=1.0, in1=c_sb[:, :, cols], op0=ALU.add, op1=ALU.mult)
                stt(out=norm[:, :, cols], in0=turn[:], scalar=1.0, in1=n_half[:, :, cols], op0=ALU.add, op1=ALU.mult)
            elif gate == G_I:
                stt(out=norm[:, :, cols], in0=turn[:], scalar=50.0, in1=norm[:, :, cols], op0=ALU.min, op1=ALU.add)
            elif gate == G_Z:
                stt(out=cell[:, :, cols], in0=cell[:, :, cols], scalar=0.5, in1=turn[:], op0=ALU.mult, op1=ALU.add)
            else:
                pair, second = divmod(c, 2)
                if not second:
                    h_tile = h_pool.tile([P, ROWS, 2 * P], F32, name="h_tile")
                    live["h_tile"] = h_tile
                own = slice(second * P, (second + 1) * P)
                if e < N_ITEMS - 2:
                    stt(out=live["h_tile"][:, :, own], in0=turn[:], scalar=1.0, in1=ratio[:, :, cols], op0=ALU.add, op1=ALU.mult)
                    if second:
                        nc.sync.dma_start(out=h_out[:, :, pair * 2 * P:(pair + 1) * 2 * P], in_=live.pop("h_tile")[:])
                else:
                    pieces = ((0, ROWS),) if e < N_ITEMS - 1 else ((0, ROWS // 2), (ROWS // 2, ROWS))
                    for t0, t1 in pieces:
                        stt(out=live["h_tile"][:, t0:t1, own], in0=turn[:, t0:t1, :], scalar=1.0, in1=ratio[:, t0:t1, cols],
                            op0=ALU.add, op1=ALU.mult)
                        nc.sync.dma_start(out=h_out[:, t0:t1, cols], in_=live["h_tile"][:, t0:t1, own])

        def scaled_cell(half):
            for c0, c1 in (((0, 2), (2, 4)), ((4, 6), (6, 7)))[half]:
                cols = slice(c0 * P, c1 * P)
                nc.vector.tensor_mul(out=ratio[:, :, cols], in0=cell[:, :, cols], in1=ratio[:, :, cols])

        def scaled_cell_on_gpsimd():
            nc.gpsimd.tensor_scalar(out=live["last_grouped"][:, 0:4, :], in0=live["last_raw"][:, :, 0:4].rearrange("p t w -> p w t"),
                                    scalar1=1.0, scalar2=0.0, op0=ALU.mult, op1=ALU.add)
            cols = slice(H - P, H)
            nc.gpsimd.tensor_tensor(out=ratio[:, :, cols], in0=cell[:, :, cols], in1=ratio[:, :, cols], op=ALU.mult)

        load_rows(0, 0)
        load_rows(0, 1)
        load_unit(0)
        nc.vector.memset(table_warmer[:], 0.0)
        nc.scalar.activation(out=table_warmer[:], in_=table_warmer[:], func=AF.Exp)
        nc.gpsimd.memset(b_rows[:], 0.0)
        make_identity(nc, ident_f32[:])
        make_identity(nc, ident_bf16[:])
        load_unit(1)
        nc.sync.dma_start(out=b_rows[0:4 * H // P, :], in_=b.rearrange("(t c) -> t c", c=P))
        load_rows(1, 0)
        load_rows(1, 1)
        load_unit(2)
        load_unit(3)
        for u in range(4, RAW_BUFS - 1):
            load_unit(u)
        load_state(0)
        load_unit(RAW_BUFS - 1)
        transpose_rows(0, 0)
        transpose_rows(0, 1)
        b_turn = turn_pool.tile([P, P], BF16, name="b_turn", tag="turn")
        nc.tensor.transpose(b_turn[:], b_rows[:], ident_bf16[:])
        transpose_rows(1, 0)
        transpose_rows(1, 1)

        for j in range(-LEAD - 1, N_ITEMS):
            u = j + LEAD
            first = u - 5
            if first % 4 == 0 and 0 <= first < N_ITEMS:
                for e in range(first, first + 4):
                    gate_function(e)
            if 0 <= u + 1 < N_UNITS and VECTOR_COLUMNS[u + 1] + GPSIMD_COLUMNS[u + 1] < STEP:
                interleave(nc.scalar.copy, u + 1, VECTOR_COLUMNS[u + 1] + GPSIMD_COLUMNS[u + 1], STEP)
            if j in (0, 8):
                halve_n(j // 8)
            if j in (0, 8):
                gpsimd_share(j + GPSIMD_LEAD)
            if j >= 0 and j % 2 == 0:
                finish_item(j)
                finish_item(j + 1)
                if gate_and_tile(j)[0] == G_Z and j % 4 == 2:
                    cols = half_columns((j // 4) % 2)
                    nc.sync.dma_start(out=c_out[:, :, cols], in_=cell[:, :, cols])
            if j == LN_SLOT:
                for k in range(2):
                    nc.scalar.activation(out=ratio[:, 2 * k:2 * k + 2, :], in_=norm[:, 2 * k:2 * k + 2, :], func=AF.Ln,
                                         bias=1e-6, scale=1.0)
            if j in EXP_SLOTS:
                cols = half_columns(EXP_SLOTS.index(j))
                nc.scalar.activation(out=ratio[:, :, cols], in_=ratio[:, :, cols], func=AF.Exp, bias=-LN_2, scale=-1.0)
            ahead = j + TURN_LEAD
            turning = 0 <= ahead < N_ITEMS and j % 2 == 0
            if turning and gate_and_tile(ahead)[0] == G_Z:
                input_times_candidate(ahead)
                input_times_candidate(ahead + 1)
            if j in SCALED_CELL_SLOTS:
                scaled_cell(SCALED_CELL_SLOTS.index(j))
            if turning:
                turn_item(ahead)
                turn_item(ahead + 1)
            copy_first = (j > 0 and j % 2 == 1) or -4 <= j < 0
            if copy_first and u < N_UNITS and VECTOR_COLUMNS[u] > 0:
                interleave(nc.vector.tensor_copy, u, 0, VECTOR_COLUMNS[u])
            next_share = j + 1 + GPSIMD_LEAD
            if j + 1 not in (0, 8) and 0 <= next_share < N_UNITS and GPSIMD_COLUMNS[next_share] > 0:
                interleave(nc.vector.tensor_copy, next_share, 0, VECTOR_COLUMNS[next_share])
                gpsimd_share_behind_copy(next_share)
                live["copied", next_share] = True
            if 0 <= u - 1 < N_UNITS:
                quantise_unit(u - 1)
                if u - 1 == N_UNITS - 1:
                    scaled_cell_on_gpsimd()
                if u - 1 in (1, 3):
                    quantise_rows(u - 2)
                    quantise_rows(u - 1)
                if u - 1 == 1:
                    nc.vector.tensor_copy(out=bias[:], in_=b_turn[:, 0:32])
                    nc.vector.tensor_scalar_mul(out=bias_half[:], in0=b_turn[:, 16:32], scalar1=0.5)
                following = u - 1 + RAW_BUFS
                if following == SECOND_STATE_LOAD_AT:
                    load_state(1)
                if following < N_UNITS:
                    load_unit(following)
                if following == N_UNITS - 1:
                    for half in range(2):
                        nc.sync.dma_start(out=n_out[:, :, half_columns(half)], in_=norm[:, :, half_columns(half)])
                if u - 1 in (1, 3):
                    multiply_pass(u - 2)
                if u - 1 not in (0, 2):
                    multiply_pass(u - 1)
            if not copy_first and 0 <= u < N_UNITS and VECTOR_COLUMNS[u] > 0 and ("copied", u) not in live:
                interleave(nc.vector.tensor_copy, u, 0, VECTOR_COLUMNS[u])
